import numpy as np
import ml_dtypes


def mxq(x, axis, fmt="e4m3"):
    dtype, down = {"e4m3": (ml_dtypes.float8_e4m3fn, 7), "e5m2": (ml_dtypes.float8_e5m2, 14)}[fmt]
    v = np.moveaxis(np.asarray(x, np.float32).astype(ml_dtypes.bfloat16).astype(np.float64), axis, -1)
    blocks = v.reshape(v.shape[:-1] + (-1, 32))
    amax = np.abs(blocks).max(-1, keepdims=True)
    byte = np.maximum(np.where(amax > 0, np.frexp(amax)[1] - 1 + 127, 0) - down, 1)
    scale = np.exp2(byte - 127.0)
    codes = (blocks / scale).astype(np.float32).astype(dtype).astype(np.float64)
    return np.moveaxis((codes * scale).reshape(v.shape), -1, axis)


WIDE = False


def mx_kscale(k):
    if not WIDE:
        return np.ones(k)
    levels = np.array([10, -10, 5, -5, 0])
    if k % 512:
        return np.exp2(np.random.permutation(np.resize(levels, k // 32))).repeat(32)
    a = np.empty((k // 512, 16))
    for p in range(k // 512):
        a[p, :8] = np.random.permutation(np.resize(levels, 8))
        for g in range(8):
            far = levels[np.abs(levels - a[p, g]) >= 10]
            a[p, g + 8] = far[np.random.randint(len(far))]
    return np.exp2(a.ravel()).repeat(32)


BF16 = ml_dtypes.bfloat16


def bf(x):
    return np.asarray(x, np.float32).astype(BF16)


def f64(x):
    return np.asarray(x).astype(np.float64)


B, A, E, P, R = 128, 8, 8192, 512, 256


def setup_inputs():
    s_src, s_edge = mx_kscale(E), mx_kscale(E)
    t = mx_kscale(P)
    s_cat = np.concatenate([s_src, s_edge])
    return {
        "image_features": bf(np.random.standard_normal((B, E)) * s_src),
        "edge_attributes": bf(np.random.standard_normal((B, A, E)) * s_edge),
        "linear_w": bf(np.random.standard_normal((P, 2 * E)) / np.sqrt(2 * E) / s_cat * t[:, None]),
        "linear_b": bf(np.random.standard_normal(P) * 0.3 * t),
        "fwd_proj": bf(np.random.standard_normal((A, P, R)) / np.sqrt(P) / t[:, None]),
    }


def reference(image_features, edge_attributes, linear_w, linear_b, fwd_proj):
    w = f64(linear_w)
    node = mxq(f64(image_features), 1, "e4m3") @ mxq(w[:, :E].T, 0, "e4m3")
    edge = (mxq(f64(edge_attributes).reshape(B * A, E), 1, "e4m3") @ mxq(w[:, E:].T, 0, "e4m3")).reshape(B, A, P)
    agg = node[:, None, :] + edge + f64(linear_b)
    rep = mxq(agg.transpose(1, 0, 2), 2, "e4m3") @ mxq(f64(fwd_proj), 1, "e4m3")
    return rep.transpose(1, 0, 2)

@@ -1,0 +1,348 @@
+from contextlib import ExitStack
+
+import concourse.mybir as mybir
+from concourse.masks import make_identity
+
+F32 = mybir.dt.float32
+BF16 = mybir.dt.bfloat16
+U32 = mybir.dt.uint32
+U8 = mybir.dt.uint8
+FP8X4 = mybir.dt.float8_e4m3fn_x4
+
+NODES = 128
+TYPES = 8
+FEATURES = 8192
+HIDDEN = 512
+REP = 256
+
+P = 128
+PACK = 4
+K_PASS = P * PACK
+PASSES = FEATURES // K_PASS
+PASS_WORDS = K_PASS // 2
+BANK = 512
+
+CHUNK_PASSES = 4
+CHUNK = CHUNK_PASSES * K_PASS
+CHUNKS = FEATURES // CHUNK
+CHUNK_WORDS = CHUNK // 2
+RAW_BUFS = 6
+
+HALF = TYPES // 2
+HALF_COLS = HALF * NODES
+HIDDEN_TILES = HIDDEN // P
+
+RUN_BLOCKS = 2
+RUNS = PASSES // RUN_BLOCKS
+LOW_RUN = RUN_BLOCKS // 2
+
+FLOPS = 2 * FEATURES * HIDDEN * (NODES + NODES * TYPES) + 2 * TYPES * NODES * HIDDEN * REP
+
+
+def tile_attributegnn_pa_k_kernel(
+    tc, image_features, edge_attributes, linear_w, linear_b, fwd_proj, out
+):
+    nc = tc.nc
+    with ExitStack() as ctx:
+        keep = ctx.enter_context(tc.tile_pool(name="keep", bufs=1))
+        raw_pool = ctx.enter_context(tc.tile_pool(name="raw", bufs=RAW_BUFS))
+        grouped_pool = ctx.enter_context(tc.tile_pool(name="grouped", bufs=2 * RUN_BLOCKS))
+        codes_pool = ctx.enter_context(tc.tile_pool(name="codes", bufs=3 * RUN_BLOCKS))
+        small_pool = ctx.enter_context(tc.tile_pool(name="small", bufs=2))
+        acc_pool = ctx.enter_context(tc.psum_pool(name="acc", bufs=1))
+        bank_pool = ctx.enter_context(tc.psum_pool(name="bank", bufs=4))
+        ctx.enter_context(tc.manual_schedule())
+
+        identity = keep.tile([P, P], F32, name="identity")
+        make_identity(nc, identity[:])
+
+        w_rows = linear_w.rearrange("(p t) k -> p t k", t=PACK)
+        order = []
+        views = {}
+        pieces_of = {}
+        for c in range(CHUNKS):
+            views["w_edge", c] = w_rows[:, :, FEATURES + c * CHUNK : FEATURES + (c + 1) * CHUNK]
+            views["edge_low", c] = edge_attributes[:, 0:HALF, c * CHUNK : (c + 1) * CHUNK]
+            order.extend([("w_edge", c), ("edge_low", c)])
+        views["image", 0] = image_features.rearrange("b (s k) -> b s k", k=CHUNK)
+        order.append(("image", 0))
+        for c in range(CHUNKS):
+            views["w_src", c] = w_rows[:, :, c * CHUNK : (c + 1) * CHUNK]
+            order.append(("w_src", c))
+        views["fwd", 0] = fwd_proj.rearrange("a (p t) r -> p a (t r)", t=PACK)
+        for c in range(CHUNKS):
+            if c == CHUNKS // 2:
+                order.append(("fwd", 0))
+            views["edge_high", c] = edge_attributes[:, HALF:TYPES, c * CHUNK : (c + 1) * CHUNK]
+            order.append(("edge_high", c))
+        for key in order:
+            pieces_of[key] = 1
+        for c in range(CHUNKS):
+            for name in ("w_edge", "edge_low"):
+                pieces_of[name, c] = CHUNK_PASSES if c == 0 else CHUNK_PASSES // 2
+
+        raws = {}
+
+        def load_next():
+            key = order[len(raws)]
+            raw = raw_pool.tile([P, PACK * CHUNK], BF16, name="raw")
+            raws[key] = raw
+            pieces = pieces_of[key]
+            source = views[key]
+            target = raw[:].rearrange("p (i s k) -> p i s k", i=pieces, s=source.shape[1])
+            width = source.shape[2] // pieces
+            return [(target[:, i], source[:, :, i * width : (i + 1) * width]) for i in range(pieces)]
+
+        def refill(count):
+            for pieces_read_together in zip(*[load_next() for i in range(count)]):
+                for target, source in pieces_read_together:
+                    nc.sync.dma_start(out=target, in_=source)
+
+        for i in range(RAW_BUFS // 2):
+            refill(2)
+        bias_bf16 = keep.tile([P, HIDDEN_TILES], BF16, name="bias_bf16")
+        nc.sync.dma_start(out=bias_bf16[:], in_=linear_b.rearrange("(p t) -> p t", t=PACK))
+
+        def tiles_of_pass(key, g_in_chunk):
+            passes_in_piece = CHUNK_PASSES // pieces_of[key]
+            piece, g_in_piece = divmod(g_in_chunk, passes_in_piece)
+            tile_step = passes_in_piece * PASS_WORDS
+            return raws[key][:].bitcast(F32), piece * PACK * tile_step + g_in_piece * PASS_WORDS, tile_step
+
+        def transpose_block(source_words, first_word, tile_step, first_bank):
+            grouped = grouped_pool.tile([P, PACK * BANK], BF16, name="grouped", align_bytes=64)
+            grouped_words = grouped[:].bitcast(F32)
+            for pair in range(2):
+                bank = bank_pool.tile([P, BANK], F32, name="bank")
+                for quarter in range(4):
+                    s, u = divmod(quarter, 2)
+                    first = first_word + (2 * pair + s) * tile_step
+                    nc.tensor.transpose(
+                        bank[:, quarter * P : (quarter + 1) * P],
+                        source_words[:, first + u : first + PASS_WORDS : 2],
+                        identity[:],
+                    )
+                target = grouped_words[:, pair * BANK : (pair + 1) * BANK].rearrange(
+                    "p (s r u) -> p s r u", s=2, u=2
+                )
+                source = bank[:].rearrange("p (s u r) -> p s r u", s=2, u=2)
+                if (first_bank + pair) % 4 == 3:
+                    nc.vector.tensor_copy(out=target, in_=source)
+                else:
+                    nc.scalar.copy(out=target, in_=source)
+            return grouped
+
+        def quantise(grouped, codes, scales):
+            nc.vector.quantize_mx(out=codes.bitcast(FP8X4), scales=scales, in_=grouped)
+
+        history = []
+
+        def advance(blocks, passes):
+            n = len(history)
+            if n >= 1:
+                for grouped, block in zip(history[n - 1][0], history[n - 1][1]):
+                    quantise(grouped[:], block[3], block[4])
+            grouped_tiles = [
+                transpose_block(block[0], block[1], block[2], 2 * i) for i, block in enumerate(blocks)
+            ]
+            history.append((grouped_tiles, blocks, passes))
+            if n >= 2 and history[n - 2][2] is not None:
+                history[n - 2][2]()
+
+        def later(passes, run):
+            return lambda: passes(run)
+
+        def new_codes():
+            codes = codes_pool.tile([P, BANK], U32, name="codes", align_bytes=64)
+            scales = codes_pool.tile([P, BANK], U8, name="scales", align_bytes=64)
+            return codes, scales
+
+        def mx(bank, lhs_codes, lhs_scales, rhs_codes, rhs_scales, g):
+            nc.tensor.matmul_mx(
+                out=bank,
+                lhsT=lhs_codes.bitcast(FP8X4),
+                lhsT_scale=lhs_scales,
+                rhs=rhs_codes.bitcast(FP8X4),
+                rhs_scale=rhs_scales,
+                start=(g == 0),
+                stop=(g == PASSES - 1),
+            )
+
+        w_edge_codes = keep.tile([P, PASSES * HIDDEN], U32, name="w_edge_codes", align_bytes=64)
+        w_edge_scales = keep.tile([P, PASSES * HIDDEN], U8, name="w_edge_scales", align_bytes=64)
+        image_codes = keep.tile([P, PASSES * NODES], U32, name="image_codes", align_bytes=64)
+        image_scales = keep.tile([P, PASSES * NODES], U8, name="image_scales", align_bytes=64)
+        fwd_codes = keep.tile([P, TYPES * REP], U32, name="fwd_codes", align_bytes=64)
+        fwd_scales = keep.tile([P, TYPES * REP], U8, name="fwd_scales", align_bytes=64)
+
+        acc = {}
+
+        def open_banks(name, run):
+            if run[0][0] == 0:
+                acc[name] = [acc_pool.tile([P, BANK], F32, name="acc%d" % t) for t in range(HIDDEN_TILES)]
+
+        def is_last(run):
+            return run[-1][0] == PASSES - 1
+
+        def edge_passes(name, run):
+            open_banks(name, run)
+            for t in range(HIDDEN_TILES):
+                for g, codes, scales in run:
+                    cols = slice(g * HIDDEN + t * P, g * HIDDEN + (t + 1) * P)
+                    mx(acc[name][t][:], w_edge_codes[:, cols], w_edge_scales[:, cols], codes[:], scales[:], g)
+
+        def second_product(agg_grouped, half):
+            agg_codes, agg_scales = new_codes()
+            quantise(agg_grouped[:], agg_codes[:], agg_scales[:])
+            for pair in range(HALF // 2):
+                bank = bank_pool.tile([P, BANK], F32, name="bank")
+                for i in range(2):
+                    a = 2 * pair + i
+                    nodes = slice(a * NODES, (a + 1) * NODES)
+                    reps = slice((half * HALF + a) * REP, (half * HALF + a + 1) * REP)
+                    nc.tensor.matmul_mx(
+                        out=bank[:, i * REP : (i + 1) * REP],
+                        lhsT=agg_codes[:, nodes].bitcast(FP8X4),
+                        lhsT_scale=agg_scales[:, nodes],
+                        rhs=fwd_codes[:, reps].bitcast(FP8X4),
+                        rhs_scale=fwd_scales[:, reps],
+                        start=True,
+                        stop=True,
+                    )
+                result = small_pool.tile([P, BANK], F32, name="result")
+                if pair % 2 == 0:
+                    nc.scalar.copy(out=result[:], in_=bank[:])
+                else:
+                    nc.vector.tensor_copy(out=result[:], in_=bank[:])
+                first_type = half * HALF + 2 * pair
+                nc.sync.dma_start(
+                    out=out[:, first_type : first_type + 2, :], in_=result[:].rearrange("b (a r) -> b a r", a=2)
+                )
+
+        parked = [keep.tile([P, BANK], F32, name="park%d" % t) for t in range(HIDDEN_TILES)]
+
+        def low_passes(run):
+            edge_passes("low", run)
+            if is_last(run):
+                for t in range(HIDDEN_TILES):
+                    if t % 2 == 0:
+                        nc.scalar.copy(out=parked[t][:], in_=acc["low"][t][:])
+                    else:
+                        nc.vector.tensor_copy(out=parked[t][:], in_=acc["low"][t][:])
+
+        bias = keep.tile([P, HIDDEN_TILES], F32, name="bias")
+        node_bias = keep.tile([P, HIDDEN_TILES * NODES], F32, name="node_bias")
+        agg_low = keep.tile([P, PACK * HALF_COLS], BF16, name="agg_low", align_bytes=64)
+
+        def node_bias_for_all_types(t):
+            return node_bias[:, t * NODES : (t + 1) * NODES].unsqueeze(1).to_broadcast([P, HALF, NODES])
+
+        def node_passes(run):
+            open_banks("node", run)
+            for t in range(HIDDEN_TILES):
+                for g, codes, scales in run:
+                    cols = slice(t * P, (t + 1) * P)
+                    nodes = slice(g * NODES, (g + 1) * NODES)
+                    mx(
+                        acc["node"][t][:, 0:NODES],
+                        codes[:, cols],
+                        scales[:, cols],
+                        image_codes[:, nodes],
+                        image_scales[:, nodes],
+                        g,
+                    )
+            if is_last(run):
+                nc.vector.tensor_copy(out=bias[:], in_=bias_bf16[:])
+                for t in range(HIDDEN_TILES):
+                    nc.scalar.activation(
+                        out=node_bias[:, t * NODES : (t + 1) * NODES],
+                        in_=acc["node"][t][:, 0:NODES],
+                        func=mybir.ActivationFunctionType.Identity,
+                        bias=bias[:, t : t + 1],
+                    )
+                for t in range(HIDDEN_TILES):
+                    nc.gpsimd.tensor_tensor(
+                        out=agg_low[:].rearrange("p (a b t) -> p t a b", a=HALF, t=PACK)[:, t],
+                        in0=parked[t][:].rearrange("p (a b) -> p a b", a=HALF),
+                        in1=node_bias_for_all_types(t),
+                        op=mybir.AluOpType.add,
+                    )
+
+        agg_rows = keep.tile([P, PACK * HALF_COLS], BF16, name="agg_rows")
+        agg_high = keep.tile([P, PACK * HALF_COLS], BF16, name="agg_high", align_bytes=64)
+
+        def high_passes(run):
+            if is_last(run):
+                second_product(agg_low, 0)
+            edge_passes("high", run)
+            if is_last(run):
+                for t in range(HIDDEN_TILES):
+                    nc.vector.tensor_tensor(
+                        out=agg_rows[:, t * HALF_COLS : (t + 1) * HALF_COLS].rearrange("p (a b) -> p a b", a=HALF),
+                        in0=acc["high"][t][:].rearrange("p (a b) -> p a b", a=HALF),
+                        in1=node_bias_for_all_types(t),
+                        op=mybir.AluOpType.add,
+                    )
+                nc.vector.tensor_copy(
+                    out=agg_high[:].rearrange("p (c t) -> p c t", t=PACK),
+                    in_=agg_rows[:].rearrange("p (t c) -> p c t", t=PACK),
+                )
+                second_product(agg_high, 1)
+
+        def stream_run(name, n, passes):
+            run = []
+            blocks = []
+            for g in range(n * RUN_BLOCKS, (n + 1) * RUN_BLOCKS):
+                c, g_in_chunk = divmod(g, CHUNK_PASSES)
+                codes, scales = new_codes()
+                run.append((g, codes, scales))
+                blocks.append(tiles_of_pass((name, c), g_in_chunk) + (codes[:], scales[:]))
+            advance(blocks, later(passes, run))
+            if (n + 1) * RUN_BLOCKS % CHUNK_PASSES == 0 and len(raws) < len(order):
+                refill(1)
+
+        for n in range(PASSES // LOW_RUN):
+            run = []
+            blocks = []
+            for g in range(n * LOW_RUN, (n + 1) * LOW_RUN):
+                c, g_in_chunk = divmod(g, CHUNK_PASSES)
+                codes, scales = new_codes()
+                run.append((g, codes, scales))
+                cols = slice(g * HIDDEN, (g + 1) * HIDDEN)
+                blocks.append(tiles_of_pass(("w_edge", c), g_in_chunk) + (w_edge_codes[:, cols], w_edge_scales[:, cols]))
+                blocks.append(tiles_of_pass(("edge_low", c), g_in_chunk) + (codes[:], scales[:]))
+            advance(blocks, later(low_passes, run))
+            if (n + 1) * LOW_RUN % CHUNK_PASSES == 0:
+                refill(2)
+
+        image_words = raws["image", 0][:].bitcast(F32)
+        for n in range(PASSES // (PACK * RUN_BLOCKS)):
+            blocks = []
+            for j in range(n * RUN_BLOCKS, (n + 1) * RUN_BLOCKS):
+                cols = slice(j * BANK, (j + 1) * BANK)
+                blocks.append((image_words, j * PACK * PASS_WORDS, PASS_WORDS, image_codes[:, cols], image_scales[:, cols]))
+            advance(blocks, None)
+        refill(1)
+
+        for n in range(RUNS):
+            stream_run("w_src", n, node_passes)
+
+        for n in range(RUNS):
+            m = n - RUNS // 2
+            types_of_run = range(m * 2 * TYPES // RUNS, (m + 1) * 2 * TYPES // RUNS) if m >= 0 else range(0)
+            fwd_grouped = {}
+            for a in types_of_run:
+                fwd_grouped[a] = small_pool.tile([P, PACK * REP], BF16, name="fwd_grouped", align_bytes=64)
+                target = fwd_grouped[a][:].rearrange("p (r t) -> p r t", t=PACK)
+                source = raws["fwd", 0][:, a * PACK * REP : (a + 1) * PACK * REP].rearrange("p (t r) -> p r t", t=PACK)
+                if a % 2 == 0:
+                    nc.scalar.copy(out=target, in_=source)
+                else:
+                    nc.vector.tensor_copy(out=target, in_=source)
+            stream_run("edge_high", n, high_passes)
+            for a in types_of_run:
+                reps = slice(a * REP, (a + 1) * REP)
+                quantise(fwd_grouped[a][:], fwd_codes[:, reps], fwd_scales[:, reps])
+
+        advance([], None)
+        advance([], None)

@@ -19,22 +19,13 @@ P = 128
 PACK = 4
 K_PASS = P * PACK
 PASSES = FEATURES // K_PASS
-PASS_WORDS = K_PASS // 2
 BANK = 512
 
-CHUNK_PASSES = 4
-CHUNK = CHUNK_PASSES * K_PASS
-CHUNKS = FEATURES // CHUNK
-CHUNK_WORDS = CHUNK // 2
-RAW_BUFS = 6
-
-HALF = TYPES // 2
-HALF_COLS = HALF * NODES
-HIDDEN_TILES = HIDDEN // P
-
-RUN_BLOCKS = 2
-RUNS = PASSES // RUN_BLOCKS
-LOW_RUN = RUN_BLOCKS // 2
+SHARE = 32
+HALF_SHARE = SHARE // 2
+PIECE = 8 * K_PASS
+RAW_BUFS = 8
+W_TILES = HIDDEN // P
 
 FLOPS = 2 * FEATURES * HIDDEN * (NODES + NODES * TYPES) + 2 * TYPES * NODES * HIDDEN * REP
 
@@ -46,303 +37,402 @@ def tile_attributegnn_pa_k_kernel(
     with ExitStack() as ctx:
         keep = ctx.enter_context(tc.tile_pool(name="keep", bufs=1))
         raw_pool = ctx.enter_context(tc.tile_pool(name="raw", bufs=RAW_BUFS))
-        grouped_pool = ctx.enter_context(tc.tile_pool(name="grouped", bufs=2 * RUN_BLOCKS))
-        codes_pool = ctx.enter_context(tc.tile_pool(name="codes", bufs=3 * RUN_BLOCKS))
+        ordered_pool = ctx.enter_context(tc.tile_pool(name="ordered", bufs=4))
+        grouped_pool = ctx.enter_context(tc.tile_pool(name="grouped", bufs=4))
+        codes_pool = ctx.enter_context(tc.tile_pool(name="codes", bufs=10))
         small_pool = ctx.enter_context(tc.tile_pool(name="small", bufs=2))
         acc_pool = ctx.enter_context(tc.psum_pool(name="acc", bufs=1))
         bank_pool = ctx.enter_context(tc.psum_pool(name="bank", bufs=4))
         ctx.enter_context(tc.manual_schedule())
 
+        bias_rows = keep.tile([P, HIDDEN], BF16, name="bias_rows")
+        nc.gpsimd.memset(bias_rows[:], 0.0)
+        ones = keep.tile([P, P], BF16, name="ones")
+        nc.gpsimd.memset(ones[:], 1.0)
+        nc.scalar.dma_start(out=bias_rows[0:1, :], in_=linear_b.rearrange("(o k) -> o k", o=1))
         identity = keep.tile([P, P], F32, name="identity")
         make_identity(nc, identity[:])
 
-        w_rows = linear_w.rearrange("(p t) k -> p t k", t=PACK)
+        w_rows = linear_w.rearrange("(i p) k -> p i k", p=P)
+        fwd_raw = keep.tile([P, TYPES * PACK * REP], BF16, name="fwd_raw")
+        fwd_rows = fwd_proj.rearrange("a (p t) r -> p a (t r)", t=PACK)
+
         order = []
-        views = {}
-        pieces_of = {}
-        for c in range(CHUNKS):
-            views["w_edge", c] = w_rows[:, :, FEATURES + c * CHUNK : FEATURES + (c + 1) * CHUNK]
-            views["edge_low", c] = edge_attributes[:, 0:HALF, c * CHUNK : (c + 1) * CHUNK]
-            order.extend([("w_edge", c), ("edge_low", c)])
-        views["image", 0] = image_features.rearrange("b (s k) -> b s k", k=CHUNK)
-        order.append(("image", 0))
-        for c in range(CHUNKS):
-            views["w_src", c] = w_rows[:, :, c * CHUNK : (c + 1) * CHUNK]
-            order.append(("w_src", c))
-        views["fwd", 0] = fwd_proj.rearrange("a (p t) r -> p a (t r)", t=PACK)
-        for c in range(CHUNKS):
-            if c == CHUNKS // 2:
-                order.append(("fwd", 0))
-            views["edge_high", c] = edge_attributes[:, HALF:TYPES, c * CHUNK : (c + 1) * CHUNK]
-            order.append(("edge_high", c))
-        for key in order:
-            pieces_of[key] = 1
-        for c in range(CHUNKS):
-            for name in ("w_edge", "edge_low"):
-                pieces_of[name, c] = CHUNK_PASSES if c == 0 else CHUNK_PASSES // 2
+        sources = {}
+        splits = {}
+
+        def piece(key, *views):
+            order.append(key)
+            sources[key] = views
+            splits[key] = 1
+
+        for m in range(PASSES // 2):
+            cols = slice(m * 2 * K_PASS, (m + 1) * 2 * K_PASS)
+            piece(("w_edge", m), w_rows[:, :, FEATURES + m * 2 * K_PASS : FEATURES + (m + 1) * 2 * K_PASS])
+            piece(("low", m), edge_attributes[:, 0:4, cols])
+        splits["w_edge", 0] = splits["low", 0] = 2
+        for c in range(PASSES // 4):
+            cols = slice(c * 4 * K_PASS, (c + 1) * 4 * K_PASS)
+            image = image_features[:, cols].rearrange("b (o k) -> b o k", o=1)
+            piece(("node", c), image, edge_attributes[:, 4:5, cols])
+            for m in (2 * c, 2 * c + 1):
+                piece(("w_src", m), w_rows[:, :, m * 2 * K_PASS : (m + 1) * 2 * K_PASS])
+        for c in range(PASSES // 4):
+            piece(("high", c), edge_attributes[:, 5:7, c * 4 * K_PASS : (c + 1) * 4 * K_PASS])
+        for c in range(PASSES // 8):
+            piece(("last", c), edge_attributes[:, 7:8, c * 8 * K_PASS : (c + 1) * 8 * K_PASS])
 
         raws = {}
+        ordered = {}
 
-        def load_next():
-            key = order[len(raws)]
-            raw = raw_pool.tile([P, PACK * CHUNK], BF16, name="raw")
+        def load_piece(key):
+            raw = raw_pool.tile([P, PIECE], BF16, name="raw")
             raws[key] = raw
-            pieces = pieces_of[key]
-            source = views[key]
-            target = raw[:].rearrange("p (i s k) -> p i s k", i=pieces, s=source.shape[1])
-            width = source.shape[2] // pieces
-            return [(target[:, i], source[:, :, i * width : (i + 1) * width]) for i in range(pieces)]
+            parts = splits[key]
+            tiles = sum(view.shape[1] for view in sources[key])
+            target = raw[:].rearrange("p (h i k) -> p h i k", h=parts, i=tiles)
+            width = PIECE // (parts * tiles)
+            dmas = []
+            for h in range(parts):
+                i = 0
+                for view in sources[key]:
+                    n = view.shape[1]
+                    dmas.append((target[:, h, i : i + n], view[:, :, h * width : (h + 1) * width]))
+                    i += n
+            return dmas
 
-        def refill(count):
-            for pieces_read_together in zip(*[load_next() for i in range(count)]):
-                for target, source in pieces_read_together:
+        def refill():
+            if len(raws) < len(order):
+                key = order[len(raws)]
+                for target, source in load_piece(key):
                     nc.sync.dma_start(out=target, in_=source)
+                if key == ("w_src", 2):
+                    load_fwd(0)
+                if key == ("w_src", 6):
+                    load_fwd(1)
 
-        for i in range(RAW_BUFS // 2):
-            refill(2)
-        bias_bf16 = keep.tile([P, HIDDEN_TILES], BF16, name="bias_bf16")
-        nc.sync.dma_start(out=bias_bf16[:], in_=linear_b.rearrange("(p t) -> p t", t=PACK))
+        def load_fwd(half):
+            width = TYPES * PACK * REP // 2
+            nc.sync.dma_start(
+                out=fwd_raw[:, half * width : (half + 1) * width].rearrange("p (a x) -> p a x", a=TYPES // 2),
+                in_=fwd_rows[:, half * TYPES // 2 : (half + 1) * TYPES // 2],
+            )
 
-        def tiles_of_pass(key, g_in_chunk):
-            passes_in_piece = CHUNK_PASSES // pieces_of[key]
-            piece, g_in_piece = divmod(g_in_chunk, passes_in_piece)
-            tile_step = passes_in_piece * PASS_WORDS
-            return raws[key][:].bitcast(F32), piece * PACK * tile_step + g_in_piece * PASS_WORDS, tile_step
+        first_w = load_piece(order[0])
+        first_e = load_piece(order[1])
+        for pair in zip(first_w, first_e):
+            for target, source in pair:
+                nc.sync.dma_start(out=target, in_=source)
+        for i in range(RAW_BUFS - 2):
+            refill()
 
-        def transpose_block(source_words, first_word, tile_step, first_bank):
+        def reorder(key, h=0):
+            parts = splits[key]
+            if h == 0:
+                ordered[key] = ordered_pool.tile([P, PIECE], BF16, name="ordered")
+            cols = slice(h * PIECE // parts, (h + 1) * PIECE // parts)
+            nc.vector.tensor_copy(
+                out=ordered[key][:, cols].rearrange("p (u n e) -> p u n e", u=2, e=HALF_SHARE),
+                in_=raws[key][:, cols].rearrange("p (n u e) -> p u n e", u=2, e=HALF_SHARE),
+            )
+
+        def reorder_next():
+            if len(ordered) < len(order):
+                reorder(order[len(ordered)])
+                refill()
+
+        def first_word(key, i, j, u):
+            tiles = sum(view.shape[1] for view in sources[key])
+            parts = splits[key]
+            part_words = PIECE // (2 * parts)
+            passes = 8 // (tiles * parts)
+            h, j = divmod(j, passes)
+            return h * part_words + u * (part_words // 2) + (i * passes + j) * P
+
+        def transpose_block(pairs):
             grouped = grouped_pool.tile([P, PACK * BANK], BF16, name="grouped", align_bytes=64)
             grouped_words = grouped[:].bitcast(F32)
-            for pair in range(2):
+            for half in range(2):
                 bank = bank_pool.tile([P, BANK], F32, name="bank")
-                for quarter in range(4):
-                    s, u = divmod(quarter, 2)
-                    first = first_word + (2 * pair + s) * tile_step
-                    nc.tensor.transpose(
-                        bank[:, quarter * P : (quarter + 1) * P],
-                        source_words[:, first + u : first + PASS_WORDS : 2],
-                        identity[:],
-                    )
-                target = grouped_words[:, pair * BANK : (pair + 1) * BANK].rearrange(
-                    "p (s r u) -> p s r u", s=2, u=2
+                for s in range(2):
+                    key, i, j = pairs[2 * half + s]
+                    words = ordered[key][:].bitcast(F32)
+                    for u in range(2):
+                        first = first_word(key, i, j, u)
+                        quarter = 2 * s + u
+                        nc.tensor.transpose(
+                            bank[:, quarter * P : (quarter + 1) * P], words[:, first : first + P], identity[:]
+                        )
+                nc.scalar.copy(
+                    out=grouped_words[:, half * BANK : (half + 1) * BANK].rearrange("p (s r u) -> p s r u", s=2, u=2),
+                    in_=bank[:].rearrange("p (s u r) -> p s r u", s=2, u=2),
                 )
-                source = bank[:].rearrange("p (s u r) -> p s r u", s=2, u=2)
-                if (first_bank + pair) % 4 == 3:
-                    nc.vector.tensor_copy(out=target, in_=source)
-                else:
-                    nc.scalar.copy(out=target, in_=source)
             return grouped
 
         def quantise(grouped, codes, scales):
             nc.vector.quantize_mx(out=codes.bitcast(FP8X4), scales=scales, in_=grouped)
 
-        history = []
-
-        def advance(blocks, passes):
-            n = len(history)
-            if n >= 1:
-                for grouped, block in zip(history[n - 1][0], history[n - 1][1]):
-                    quantise(grouped[:], block[3], block[4])
-            grouped_tiles = [
-                transpose_block(block[0], block[1], block[2], 2 * i) for i, block in enumerate(blocks)
-            ]
-            history.append((grouped_tiles, blocks, passes))
-            if n >= 2 and history[n - 2][2] is not None:
-                history[n - 2][2]()
-
-        def later(passes, run):
-            return lambda: passes(run)
-
         def new_codes():
             codes = codes_pool.tile([P, BANK], U32, name="codes", align_bytes=64)
             scales = codes_pool.tile([P, BANK], U8, name="scales", align_bytes=64)
-            return codes, scales
+            return codes[:], scales[:]
 
-        def mx(bank, lhs_codes, lhs_scales, rhs_codes, rhs_scales, g):
+        def mx(bank, lhs, rhs, start, stop):
             nc.tensor.matmul_mx(
                 out=bank,
-                lhsT=lhs_codes.bitcast(FP8X4),
-                lhsT_scale=lhs_scales,
-                rhs=rhs_codes.bitcast(FP8X4),
-                rhs_scale=rhs_scales,
-                start=(g == 0),
-                stop=(g == PASSES - 1),
+                lhsT=lhs[0].bitcast(FP8X4),
+                lhsT_scale=lhs[1],
+                rhs=rhs[0].bitcast(FP8X4),
+                rhs_scale=rhs[1],
+                start=start,
+                stop=stop,
             )
+
+        def columns(pair, first, width):
+            return pair[0][:, first : first + width], pair[1][:, first : first + width]
 
         w_edge_codes = keep.tile([P, PASSES * HIDDEN], U32, name="w_edge_codes", align_bytes=64)
         w_edge_scales = keep.tile([P, PASSES * HIDDEN], U8, name="w_edge_scales", align_bytes=64)
-        image_codes = keep.tile([P, PASSES * NODES], U32, name="image_codes", align_bytes=64)
-        image_scales = keep.tile([P, PASSES * NODES], U8, name="image_scales", align_bytes=64)
+        w_edge = (w_edge_codes, w_edge_scales)
         fwd_codes = keep.tile([P, TYPES * REP], U32, name="fwd_codes", align_bytes=64)
         fwd_scales = keep.tile([P, TYPES * REP], U8, name="fwd_scales", align_bytes=64)
+        fwd = (fwd_codes, fwd_scales)
 
         acc = {}
 
-        def open_banks(name, run):
-            if run[0][0] == 0:
-                acc[name] = [acc_pool.tile([P, BANK], F32, name="acc%d" % t) for t in range(HIDDEN_TILES)]
+        def accumulate(name, slot, lhs, rhs, g):
+            if g == 0:
+                acc[name] = acc_pool.tile([P, BANK], F32, name="acc%d" % slot)
+            mx(acc[name][:], lhs, rhs, g == 0, g == PASSES - 1)
 
-        def is_last(run):
-            return run[-1][0] == PASSES - 1
+        def edge_pass(a, slot, edge, g):
+            accumulate(a, slot, edge, columns(w_edge, g * HIDDEN, HIDDEN), g)
 
-        def edge_passes(name, run):
-            open_banks(name, run)
-            for t in range(HIDDEN_TILES):
-                for g, codes, scales in run:
-                    cols = slice(g * HIDDEN + t * P, g * HIDDEN + (t + 1) * P)
-                    mx(acc[name][t][:], w_edge_codes[:, cols], w_edge_scales[:, cols], codes[:], scales[:], g)
+        runs = []
+        for g in range(PASSES):
+            m, j = divmod(g, 2)
+            edges = {}
 
-        def second_product(agg_grouped, half):
-            agg_codes, agg_scales = new_codes()
-            quantise(agg_grouped[:], agg_codes[:], agg_scales[:])
-            for pair in range(HALF // 2):
-                bank = bank_pool.tile([P, BANK], F32, name="bank")
-                for i in range(2):
-                    a = 2 * pair + i
-                    nodes = slice(a * NODES, (a + 1) * NODES)
-                    reps = slice((half * HALF + a) * REP, (half * HALF + a + 1) * REP)
-                    nc.tensor.matmul_mx(
-                        out=bank[:, i * REP : (i + 1) * REP],
-                        lhsT=agg_codes[:, nodes].bitcast(FP8X4),
-                        lhsT_scale=agg_scales[:, nodes],
-                        rhs=fwd_codes[:, reps].bitcast(FP8X4),
-                        rhs_scale=fwd_scales[:, reps],
-                        start=True,
-                        stop=True,
-                    )
-                result = small_pool.tile([P, BANK], F32, name="result")
-                if pair % 2 == 0:
-                    nc.scalar.copy(out=result[:], in_=bank[:])
-                else:
-                    nc.vector.tensor_copy(out=result[:], in_=bank[:])
-                first_type = half * HALF + 2 * pair
-                nc.sync.dma_start(
-                    out=out[:, first_type : first_type + 2, :], in_=result[:].rearrange("b (a r) -> b a r", a=2)
+            def low_passes(g=g, edges=edges):
+                for a in range(4):
+                    edge_pass(a, a, columns(edges["codes"], a * P, P), g)
+
+            runs.append(
+                (
+                    [
+                        ([(("w_edge", m), i, j) for i in range(4)], g, None),
+                        ([(("low", m), i, j) for i in range(4)], None, edges),
+                    ],
+                    low_passes,
                 )
+            )
+        for c in range(PASSES // 4):
+            images = {}
+            fours = {}
 
-        parked = [keep.tile([P, BANK], F32, name="park%d" % t) for t in range(HIDDEN_TILES)]
+            def four_passes(c=c, fours=fours):
+                for j in range(4):
+                    edge_pass(4, 1, columns(fours["codes"], j * P, P), 4 * c + j)
 
-        def low_passes(run):
-            edge_passes("low", run)
-            if is_last(run):
-                for t in range(HIDDEN_TILES):
-                    if t % 2 == 0:
-                        nc.scalar.copy(out=parked[t][:], in_=acc["low"][t][:])
-                    else:
-                        nc.vector.tensor_copy(out=parked[t][:], in_=acc["low"][t][:])
-
-        bias = keep.tile([P, HIDDEN_TILES], F32, name="bias")
-        node_bias = keep.tile([P, HIDDEN_TILES * NODES], F32, name="node_bias")
-        agg_low = keep.tile([P, PACK * HALF_COLS], BF16, name="agg_low", align_bytes=64)
-
-        def node_bias_for_all_types(t):
-            return node_bias[:, t * NODES : (t + 1) * NODES].unsqueeze(1).to_broadcast([P, HALF, NODES])
-
-        def node_passes(run):
-            open_banks("node", run)
-            for t in range(HIDDEN_TILES):
-                for g, codes, scales in run:
-                    cols = slice(t * P, (t + 1) * P)
-                    nodes = slice(g * NODES, (g + 1) * NODES)
-                    mx(
-                        acc["node"][t][:, 0:NODES],
-                        codes[:, cols],
-                        scales[:, cols],
-                        image_codes[:, nodes],
-                        image_scales[:, nodes],
-                        g,
-                    )
-            if is_last(run):
-                nc.vector.tensor_copy(out=bias[:], in_=bias_bf16[:])
-                for t in range(HIDDEN_TILES):
-                    nc.scalar.activation(
-                        out=node_bias[:, t * NODES : (t + 1) * NODES],
-                        in_=acc["node"][t][:, 0:NODES],
-                        func=mybir.ActivationFunctionType.Identity,
-                        bias=bias[:, t : t + 1],
-                    )
-                for t in range(HIDDEN_TILES):
-                    nc.gpsimd.tensor_tensor(
-                        out=agg_low[:].rearrange("p (a b t) -> p t a b", a=HALF, t=PACK)[:, t],
-                        in0=parked[t][:].rearrange("p (a b) -> p a b", a=HALF),
-                        in1=node_bias_for_all_types(t),
-                        op=mybir.AluOpType.add,
-                    )
-
-        agg_rows = keep.tile([P, PACK * HALF_COLS], BF16, name="agg_rows")
-        agg_high = keep.tile([P, PACK * HALF_COLS], BF16, name="agg_high", align_bytes=64)
-
-        def high_passes(run):
-            if is_last(run):
-                second_product(agg_low, 0)
-            edge_passes("high", run)
-            if is_last(run):
-                for t in range(HIDDEN_TILES):
-                    nc.vector.tensor_tensor(
-                        out=agg_rows[:, t * HALF_COLS : (t + 1) * HALF_COLS].rearrange("p (a b) -> p a b", a=HALF),
-                        in0=acc["high"][t][:].rearrange("p (a b) -> p a b", a=HALF),
-                        in1=node_bias_for_all_types(t),
-                        op=mybir.AluOpType.add,
-                    )
-                nc.vector.tensor_copy(
-                    out=agg_high[:].rearrange("p (c t) -> p c t", t=PACK),
-                    in_=agg_rows[:].rearrange("p (t c) -> p c t", t=PACK),
+            runs.append(
+                (
+                    [
+                        ([(("node", c), 0, j) for j in range(4)], None, images),
+                        ([(("node", c), 1, j) for j in range(4)], None, fours),
+                    ],
+                    four_passes,
                 )
-                second_product(agg_high, 1)
+            )
+            for m in range(2):
+                ws = [{}, {}]
 
-        def stream_run(name, n, passes):
-            run = []
-            blocks = []
-            for g in range(n * RUN_BLOCKS, (n + 1) * RUN_BLOCKS):
-                c, g_in_chunk = divmod(g, CHUNK_PASSES)
-                codes, scales = new_codes()
-                run.append((g, codes, scales))
-                blocks.append(tiles_of_pass((name, c), g_in_chunk) + (codes[:], scales[:]))
-            advance(blocks, later(passes, run))
-            if (n + 1) * RUN_BLOCKS % CHUNK_PASSES == 0 and len(raws) < len(order):
-                refill(1)
+                def node_passes(c=c, m=m, ws=ws, images=images):
+                    for j in range(2):
+                        accumulate(
+                            "node", 0, columns(images["codes"], (2 * m + j) * P, P), ws[j]["codes"], 4 * c + 2 * m + j
+                        )
 
-        for n in range(PASSES // LOW_RUN):
-            run = []
-            blocks = []
-            for g in range(n * LOW_RUN, (n + 1) * LOW_RUN):
-                c, g_in_chunk = divmod(g, CHUNK_PASSES)
-                codes, scales = new_codes()
-                run.append((g, codes, scales))
-                cols = slice(g * HIDDEN, (g + 1) * HIDDEN)
-                blocks.append(tiles_of_pass(("w_edge", c), g_in_chunk) + (w_edge_codes[:, cols], w_edge_scales[:, cols]))
-                blocks.append(tiles_of_pass(("edge_low", c), g_in_chunk) + (codes[:], scales[:]))
-            advance(blocks, later(low_passes, run))
-            if (n + 1) * LOW_RUN % CHUNK_PASSES == 0:
-                refill(2)
+                runs.append(
+                    ([([(("w_src", 2 * c + m), i, j) for i in range(4)], None, ws[j]) for j in range(2)], node_passes)
+                )
+        for c in range(PASSES // 4):
+            pairs = [{}, {}]
 
-        image_words = raws["image", 0][:].bitcast(F32)
-        for n in range(PASSES // (PACK * RUN_BLOCKS)):
-            blocks = []
-            for j in range(n * RUN_BLOCKS, (n + 1) * RUN_BLOCKS):
-                cols = slice(j * BANK, (j + 1) * BANK)
-                blocks.append((image_words, j * PACK * PASS_WORDS, PASS_WORDS, image_codes[:, cols], image_scales[:, cols]))
-            advance(blocks, None)
-        refill(1)
+            def high_passes(c=c, pairs=pairs):
+                for s in range(2):
+                    for j in range(4):
+                        edge_pass(5 + s, 2 + s, columns(pairs[s]["codes"], j * P, P), 4 * c + j)
 
-        for n in range(RUNS):
-            stream_run("w_src", n, node_passes)
+            runs.append(([([(("high", c), s, j) for j in range(4)], None, pairs[s]) for s in range(2)], high_passes))
+        for c in range(PASSES // 8):
+            pairs = [{}, {}]
 
-        for n in range(RUNS):
-            m = n - RUNS // 2
-            types_of_run = range(m * 2 * TYPES // RUNS, (m + 1) * 2 * TYPES // RUNS) if m >= 0 else range(0)
-            fwd_grouped = {}
-            for a in types_of_run:
-                fwd_grouped[a] = small_pool.tile([P, PACK * REP], BF16, name="fwd_grouped", align_bytes=64)
-                target = fwd_grouped[a][:].rearrange("p (r t) -> p r t", t=PACK)
-                source = raws["fwd", 0][:, a * PACK * REP : (a + 1) * PACK * REP].rearrange("p (t r) -> p r t", t=PACK)
+            def last_passes(c=c, pairs=pairs):
+                for h in range(2):
+                    for j in range(4):
+                        edge_pass(7, 1, columns(pairs[h]["codes"], j * P, P), 8 * c + 4 * h + j)
+
+            runs.append(
+                ([([(("last", c), 0, 4 * h + j) for j in range(4)], None, pairs[h]) for h in range(2)], last_passes)
+            )
+
+        parked = [keep.tile([P, HIDDEN], F32, name="park%d" % a) for a in range(4)]
+        bias = keep.tile([P, HIDDEN], F32, name="bias")
+        node_bias = keep.tile([P, HIDDEN], F32, name="node_bias")
+
+        def park():
+            for a in range(4):
                 if a % 2 == 0:
-                    nc.scalar.copy(out=target, in_=source)
+                    nc.scalar.copy(out=parked[a][:], in_=acc[a][:])
                 else:
-                    nc.vector.tensor_copy(out=target, in_=source)
-            stream_run("edge_high", n, high_passes)
-            for a in types_of_run:
-                reps = slice(a * REP, (a + 1) * REP)
-                quantise(fwd_grouped[a][:], fwd_codes[:, reps], fwd_scales[:, reps])
+                    nc.vector.tensor_copy(out=parked[a][:], in_=acc[a][:])
 
-        advance([], None)
-        advance([], None)
+        def add_node():
+            nc.vector.tensor_tensor(out=node_bias[:], in0=acc["node"][:], in1=bias[:], op=mybir.AluOpType.add)
+
+        agg = {}
+        agg_grouped = {}
+        agg_codes = {}
+
+        def add_agg(a):
+            agg[a] = small_pool.tile([P, HIDDEN], BF16, name="agg%d" % (a % 2))
+            source = parked[a] if a < 4 else acc[a]
+            nc.vector.tensor_tensor(out=agg[a][:], in0=source[:], in1=node_bias[:], op=mybir.AluOpType.add)
+
+        def transpose_agg(types, bank):
+            n = len(types)
+            for s in range(n):
+                words = agg[types[s]][:].bitcast(F32)
+                for u in range(2):
+                    quarter = 2 * s + u
+                    nc.tensor.transpose(
+                        bank[:, quarter * P : (quarter + 1) * P], words[:, u : HIDDEN // 2 : 2], identity[:]
+                    )
+            grouped = small_pool.tile([P, 2 * PACK * P], BF16, name="agg_grouped", align_bytes=64)
+            agg_grouped[types] = grouped
+            nc.scalar.copy(
+                out=grouped[:].bitcast(F32)[:, 0 : n * 2 * P].rearrange("p (s r u) -> p s r u", s=n, u=2),
+                in_=bank[:, 0 : n * 2 * P].rearrange("p (s u r) -> p s r u", s=n, u=2),
+            )
+
+        def quantise_agg(types):
+            n = len(types)
+            codes = small_pool.tile([P, 2 * P], U32, name="agg_codes", align_bytes=64)
+            scales = small_pool.tile([P, 2 * P], U8, name="agg_scales", align_bytes=64)
+            agg_codes[types] = (codes, scales)
+            quantise(agg_grouped[types][:, 0 : n * PACK * P], codes[:, 0 : n * P], scales[:, 0 : n * P])
+
+        def second_product(types):
+            n = len(types)
+            bank = bank_pool.tile([P, BANK], F32, name="bank")
+            for s in range(n):
+                mx(
+                    bank[:, s * REP : (s + 1) * REP],
+                    columns(agg_codes[types], s * P, P),
+                    columns(fwd, types[s] * REP, REP),
+                    True,
+                    True,
+                )
+            result = small_pool.tile([P, BANK], F32, name="result")
+            nc.scalar.copy(out=result[:, 0 : n * REP], in_=bank[:, 0 : n * REP])
+            nc.sync.dma_start(
+                out=out[:, types[0] : types[0] + n, :],
+                in_=result[:, 0 : n * REP].rearrange("b (a r) -> b a r", a=n),
+            )
+
+        fwd_grouped = {}
+
+        def interleave_fwd(a):
+            fwd_grouped[a] = small_pool.tile([P, PACK * REP], BF16, name="fwd_grouped", align_bytes=64)
+            target = fwd_grouped[a][:].rearrange("p (r t) -> p r t", t=PACK)
+            source = fwd_raw[:, a * PACK * REP : (a + 1) * PACK * REP].rearrange("p (t r) -> p r t", t=PACK)
+            if a % 2 == 0:
+                nc.scalar.copy(out=target, in_=source)
+            else:
+                nc.vector.tensor_copy(out=target, in_=source)
+
+        def quantise_fwd(a):
+            fwd_cols = columns(fwd, a * REP, REP)
+            quantise(fwd_grouped[a][:], fwd_cols[0], fwd_cols[1])
+
+        def agg_bank():
+            return acc_pool.tile([P, BANK], F32, name="acc0")
+
+        for h in range(2):
+            reorder(order[0], h)
+            reorder(order[1], h)
+        refill()
+        refill()
+
+        LOW = PASSES
+        NODE_END = LOW + 3 * (PASSES // 4) + 1
+        TOTAL = len(runs)
+        pending = []
+        fwd_step = {}
+        for a in range(TYPES):
+            fwd_step[NODE_END - 3 + a] = a
+
+        for n in range(TOTAL + 2):
+            if n - 1 in fwd_step:
+                quantise_fwd(fwd_step[n - 1])
+            for grouped, codes, scales in pending:
+                quantise(grouped[:], codes, scales)
+            pending = []
+            if n < TOTAL:
+                for pairs, w_pass, place in runs[n][0]:
+                    grouped = transpose_block(pairs)
+                    if place is None:
+                        codes, scales = columns(w_edge, w_pass * HIDDEN, HIDDEN)
+                    else:
+                        codes, scales = place["codes"] = new_codes()
+                    pending.append((grouped, codes, scales))
+            e = n - NODE_END
+            if e == 1:
+                add_agg(0)
+                add_agg(1)
+            if e == 2:
+                add_agg(2)
+                add_agg(3)
+            if e == 3:
+                add_agg(4)
+            if e == 5:
+                add_agg(5)
+                add_agg(6)
+            reorder_next()
+            if n in fwd_step:
+                interleave_fwd(fwd_step[n])
+            if e == 2:
+                quantise_agg((0, 1))
+            if e == 3:
+                quantise_agg((2, 3))
+            if e == 4:
+                quantise_agg((4,))
+            if n >= 2:
+                runs[n - 2][1]()
+            if n == LOW:
+                bank = bank_pool.tile([P, BANK], F32, name="bank")
+                nc.tensor.matmul(bank[:], lhsT=ones[:], rhs=bias_rows[:], start=True, stop=True)
+                nc.scalar.copy(out=bias[:], in_=bank[:])
+            if n == LOW + 1:
+                park()
+            if e == 0:
+                add_node()
+            if e == 1:
+                transpose_agg((0, 1), agg_bank())
+            if e == 2:
+                transpose_agg((2, 3), agg_bank())
+            if e == 3:
+                second_product((0, 1))
+                transpose_agg((4,), agg_bank())
+            if e == 4:
+                second_product((2, 3))
+            if e == 5:
+                second_product((4,))
+                transpose_agg((5, 6), agg_bank())
+                quantise_agg((5, 6))
+            if e == 6:
+                add_agg(7)
+                second_product((5, 6))
+                transpose_agg((7,), agg_bank())
+                quantise_agg((7,))
+                second_product((7,))

@@ -23,9 +23,9 @@ BANK = 512
 
 SHARE = 32
 HALF_SHARE = SHARE // 2
-PIECE = 8 * K_PASS
-RAW_BUFS = 8
-W_TILES = HIDDEN // P
+BLOCK = 4 * K_PASS
+PIECE = 2 * BLOCK
+RAW_BUFS = 9
 
 FLOPS = 2 * FEATURES * HIDDEN * (NODES + NODES * TYPES) + 2 * TYPES * NODES * HIDDEN * REP
 
@@ -37,10 +37,11 @@ def tile_attributegnn_pa_k_kernel(
     with ExitStack() as ctx:
         keep = ctx.enter_context(tc.tile_pool(name="keep", bufs=1))
         raw_pool = ctx.enter_context(tc.tile_pool(name="raw", bufs=RAW_BUFS))
-        ordered_pool = ctx.enter_context(tc.tile_pool(name="ordered", bufs=4))
-        grouped_pool = ctx.enter_context(tc.tile_pool(name="grouped", bufs=4))
-        codes_pool = ctx.enter_context(tc.tile_pool(name="codes", bufs=10))
+        ordered_pool = ctx.enter_context(tc.tile_pool(name="ordered", bufs=7))
+        grouped_pool = ctx.enter_context(tc.tile_pool(name="grouped", bufs=6))
+        codes_pool = ctx.enter_context(tc.tile_pool(name="codes", bufs=12))
         small_pool = ctx.enter_context(tc.tile_pool(name="small", bufs=2))
+        fwd_pool = ctx.enter_context(tc.tile_pool(name="fwd", bufs=3))
         acc_pool = ctx.enter_context(tc.psum_pool(name="acc", bufs=1))
         bank_pool = ctx.enter_context(tc.psum_pool(name="bank", bufs=4))
         ctx.enter_context(tc.manual_schedule())
@@ -54,23 +55,22 @@ def tile_attributegnn_pa_k_kernel(
         make_identity(nc, identity[:])
 
         w_rows = linear_w.rearrange("(i p) k -> p i k", p=P)
-        fwd_raw = keep.tile([P, TYPES * PACK * REP], BF16, name="fwd_raw")
         fwd_rows = fwd_proj.rearrange("a (p t) r -> p a (t r)", t=PACK)
 
         order = []
         sources = {}
-        splits = {}
+        halved = {}
 
         def piece(key, *views):
             order.append(key)
             sources[key] = views
-            splits[key] = 1
+            halved[key] = False
 
         for m in range(PASSES // 2):
             cols = slice(m * 2 * K_PASS, (m + 1) * 2 * K_PASS)
             piece(("w_edge", m), w_rows[:, :, FEATURES + m * 2 * K_PASS : FEATURES + (m + 1) * 2 * K_PASS])
             piece(("low", m), edge_attributes[:, 0:4, cols])
-        splits["w_edge", 0] = splits["low", 0] = 2
+            halved["w_edge", m] = halved["low", m] = m < 2
         for c in range(PASSES // 4):
             cols = slice(c * 4 * K_PASS, (c + 1) * 4 * K_PASS)
             image = image_features[:, cols].rearrange("b (o k) -> b o k", o=1)
@@ -81,14 +81,15 @@ def tile_attributegnn_pa_k_kernel(
             piece(("high", c), edge_attributes[:, 5:7, c * 4 * K_PASS : (c + 1) * 4 * K_PASS])
         for c in range(PASSES // 8):
             piece(("last", c), edge_attributes[:, 7:8, c * 8 * K_PASS : (c + 1) * 8 * K_PASS])
+        for h in range(2):
+            piece(("fwd", h), fwd_rows[:, h * TYPES // 2 : (h + 1) * TYPES // 2])
 
         raws = {}
-        ordered = {}
 
         def load_piece(key):
             raw = raw_pool.tile([P, PIECE], BF16, name="raw")
             raws[key] = raw
-            parts = splits[key]
+            parts = 2 if halved[key] else 1
             tiles = sum(view.shape[1] for view in sources[key])
             target = raw[:].rearrange("p (h i k) -> p h i k", h=parts, i=tiles)
             width = PIECE // (parts * tiles)
@@ -101,65 +102,43 @@ def tile_attributegnn_pa_k_kernel(
                     i += n
             return dmas
 
-        def refill():
-            if len(raws) < len(order):
-                key = order[len(raws)]
-                for target, source in load_piece(key):
+        def refill(count):
+            dmas = [load_piece(order[len(raws)]) for i in range(count) if len(raws) < len(order)]
+            for together in zip(*dmas):
+                for target, source in together:
                     nc.sync.dma_start(out=target, in_=source)
-                if key == ("w_src", 2):
-                    load_fwd(0)
-                if key == ("w_src", 6):
-                    load_fwd(1)
 
-        def load_fwd(half):
-            width = TYPES * PACK * REP // 2
-            nc.sync.dma_start(
-                out=fwd_raw[:, half * width : (half + 1) * width].rearrange("p (a x) -> p a x", a=TYPES // 2),
-                in_=fwd_rows[:, half * TYPES // 2 : (half + 1) * TYPES // 2],
-            )
+        refill(2)
+        refill(2)
+        for i in range(RAW_BUFS - 4):
+            refill(1)
 
-        first_w = load_piece(order[0])
-        first_e = load_piece(order[1])
-        for pair in zip(first_w, first_e):
-            for target, source in pair:
-                nc.sync.dma_start(out=target, in_=source)
-        for i in range(RAW_BUFS - 2):
-            refill()
+        def raw_block(key, j):
+            raw = raws[key]
+            if key[0] in ("w_edge", "low", "w_src"):
+                pattern = "p (j s n u e) -> p j s n u e" if halved[key] else "p (s j n u e) -> p j s n u e"
+                return raw[:].rearrange(pattern, j=2, s=4, u=2, e=HALF_SHARE)[:, j]
+            return raw[:].rearrange("p (j s n u e) -> p j s n u e", j=2, s=4, u=2, e=HALF_SHARE)[:, j]
 
-        def reorder(key, h=0):
-            parts = splits[key]
-            if h == 0:
-                ordered[key] = ordered_pool.tile([P, PIECE], BF16, name="ordered")
-            cols = slice(h * PIECE // parts, (h + 1) * PIECE // parts)
+        reordered = []
+
+        def reorder(key, j):
+            ordered = ordered_pool.tile([P, BLOCK], BF16, name="ordered")
             nc.vector.tensor_copy(
-                out=ordered[key][:, cols].rearrange("p (u n e) -> p u n e", u=2, e=HALF_SHARE),
-                in_=raws[key][:, cols].rearrange("p (n u e) -> p u n e", u=2, e=HALF_SHARE),
+                out=ordered[:].rearrange("p (u s n e) -> p u s n e", u=2, s=4, e=HALF_SHARE),
+                in_=raw_block(key, j).rearrange("p s n u e -> p u s n e"),
             )
+            reordered.append(ordered)
 
-        def reorder_next():
-            if len(ordered) < len(order):
-                reorder(order[len(ordered)])
-                refill()
-
-        def first_word(key, i, j, u):
-            tiles = sum(view.shape[1] for view in sources[key])
-            parts = splits[key]
-            part_words = PIECE // (2 * parts)
-            passes = 8 // (tiles * parts)
-            h, j = divmod(j, passes)
-            return h * part_words + u * (part_words // 2) + (i * passes + j) * P
-
-        def transpose_block(pairs):
+        def transpose_block(words):
             grouped = grouped_pool.tile([P, PACK * BANK], BF16, name="grouped", align_bytes=64)
             grouped_words = grouped[:].bitcast(F32)
             for half in range(2):
                 bank = bank_pool.tile([P, BANK], F32, name="bank")
                 for s in range(2):
-                    key, i, j = pairs[2 * half + s]
-                    words = ordered[key][:].bitcast(F32)
                     for u in range(2):
-                        first = first_word(key, i, j, u)
                         quarter = 2 * s + u
+                        first = (4 * u + 2 * half + s) * P
                         nc.tensor.transpose(
                             bank[:, quarter * P : (quarter + 1) * P], words[:, first : first + P], identity[:]
                         )
@@ -208,73 +187,57 @@ def tile_attributegnn_pa_k_kernel(
         def edge_pass(a, slot, edge, g):
             accumulate(a, slot, edge, columns(w_edge, g * HIDDEN, HIDDEN), g)
 
-        runs = []
+        blocks = []
+        units = {}
+
+        def low_pass(g, edges):
+            for a in range(4):
+                edge_pass(a, a, columns(edges["codes"], a * P, P), g)
+
+        def type_passes(a, slot, codes, first):
+            for j in range(PACK):
+                edge_pass(a, slot, columns(codes["codes"], j * P, P), first + j)
+
+        def node_pass(g, images, ws):
+            accumulate("node", 0, columns(images["codes"], g % 4 * P, P), ws["codes"], g)
+
+        def block(key, j, place, unit, *args):
+            if unit is not None:
+                units[len(blocks)] = lambda: unit(*args)
+            blocks.append((key, j, place))
+
         for g in range(PASSES):
-            m, j = divmod(g, 2)
             edges = {}
-
-            def low_passes(g=g, edges=edges):
-                for a in range(4):
-                    edge_pass(a, a, columns(edges["codes"], a * P, P), g)
-
-            runs.append(
-                (
-                    [
-                        ([(("w_edge", m), i, j) for i in range(4)], g, None),
-                        ([(("low", m), i, j) for i in range(4)], None, edges),
-                    ],
-                    low_passes,
-                )
-            )
+            block(("w_edge", g // 2), g % 2, {"codes": columns(w_edge, g * HIDDEN, HIDDEN)}, None)
+            block(("low", g // 2), g % 2, edges, low_pass, g, edges)
+        LOW_BLOCKS = len(blocks)
         for c in range(PASSES // 4):
             images = {}
             fours = {}
-
-            def four_passes(c=c, fours=fours):
-                for j in range(4):
-                    edge_pass(4, 1, columns(fours["codes"], j * P, P), 4 * c + j)
-
-            runs.append(
-                (
-                    [
-                        ([(("node", c), 0, j) for j in range(4)], None, images),
-                        ([(("node", c), 1, j) for j in range(4)], None, fours),
-                    ],
-                    four_passes,
-                )
-            )
-            for m in range(2):
-                ws = [{}, {}]
-
-                def node_passes(c=c, m=m, ws=ws, images=images):
-                    for j in range(2):
-                        accumulate(
-                            "node", 0, columns(images["codes"], (2 * m + j) * P, P), ws[j]["codes"], 4 * c + 2 * m + j
-                        )
-
-                runs.append(
-                    ([([(("w_src", 2 * c + m), i, j) for i in range(4)], None, ws[j]) for j in range(2)], node_passes)
-                )
+            block(("node", c), 0, images, None)
+            block(("node", c), 1, fours, type_passes, 4, 1, fours, 4 * c)
+            for g in range(4 * c, 4 * c + 4):
+                ws = {}
+                block(("w_src", g // 2), g % 2, ws, node_pass, g, images, ws)
+        NODE_BLOCKS = len(blocks)
         for c in range(PASSES // 4):
-            pairs = [{}, {}]
-
-            def high_passes(c=c, pairs=pairs):
-                for s in range(2):
-                    for j in range(4):
-                        edge_pass(5 + s, 2 + s, columns(pairs[s]["codes"], j * P, P), 4 * c + j)
-
-            runs.append(([([(("high", c), s, j) for j in range(4)], None, pairs[s]) for s in range(2)], high_passes))
+            for s in range(2):
+                edges = {}
+                block(("high", c), s, edges, type_passes, 5 + s, 2 + s, edges, 4 * c)
+        HIGH_BLOCKS = len(blocks)
         for c in range(PASSES // 8):
-            pairs = [{}, {}]
+            for h in range(2):
+                edges = {}
+                block(("last", c), h, edges, type_passes, 7, 1, edges, 8 * c + 4 * h)
 
-            def last_passes(c=c, pairs=pairs):
-                for h in range(2):
-                    for j in range(4):
-                        edge_pass(7, 1, columns(pairs[h]["codes"], j * P, P), 8 * c + 4 * h + j)
+        RUNS = [1, 1, 2, 2, 2] + [3] * 8 + [3] * 8 + [3] * 4
+        FWD_VECTOR = (1, 3)
+        FWD_INTERLEAVE = {1: (0, 1), 2: (2, 3, 4), 3: (5, 6, 7)}
+        FWD_QUANTISE = {2: (0, 1), 3: (2, 3, 4), 4: (5, 6, 7)}
+        starts = [sum(RUNS[:n]) for n in range(len(RUNS) + 1)]
 
-            runs.append(
-                ([([(("last", c), 0, 4 * h + j) for j in range(4)], None, pairs[h]) for h in range(2)], last_passes)
-            )
+        def run_of(b):
+            return max(n for n in range(len(RUNS)) if starts[n] <= b)
 
         parked = [keep.tile([P, HIDDEN], F32, name="park%d" % a) for a in range(4)]
         bias = keep.tile([P, HIDDEN], F32, name="bias")
@@ -299,8 +262,9 @@ def tile_attributegnn_pa_k_kernel(
             source = parked[a] if a < 4 else acc[a]
             nc.vector.tensor_tensor(out=agg[a][:], in0=source[:], in1=node_bias[:], op=mybir.AluOpType.add)
 
-        def transpose_agg(types, bank):
+        def transpose_agg(types):
             n = len(types)
+            bank = bank_pool.tile([P, BANK], F32, name="bank")
             for s in range(n):
                 words = agg[types[s]][:].bitcast(F32)
                 for u in range(2):
@@ -343,10 +307,11 @@ def tile_attributegnn_pa_k_kernel(
         fwd_grouped = {}
 
         def interleave_fwd(a):
-            fwd_grouped[a] = small_pool.tile([P, PACK * REP], BF16, name="fwd_grouped", align_bytes=64)
+            fwd_grouped[a] = fwd_pool.tile([P, PACK * REP], BF16, name="fwd_grouped", align_bytes=64)
             target = fwd_grouped[a][:].rearrange("p (r t) -> p r t", t=PACK)
-            source = fwd_raw[:, a * PACK * REP : (a + 1) * PACK * REP].rearrange("p (t r) -> p r t", t=PACK)
-            if a % 2 == 0:
+            h, i = divmod(a, TYPES // 2)
+            source = raws["fwd", h][:, i * PACK * REP : (i + 1) * PACK * REP].rearrange("p (t r) -> p r t", t=PACK)
+            if a not in FWD_VECTOR:
                 nc.scalar.copy(out=target, in_=source)
             else:
                 nc.vector.tensor_copy(out=target, in_=source)
@@ -355,84 +320,87 @@ def tile_attributegnn_pa_k_kernel(
             fwd_cols = columns(fwd, a * REP, REP)
             quantise(fwd_grouped[a][:], fwd_cols[0], fwd_cols[1])
 
-        def agg_bank():
-            return acc_pool.tile([P, BANK], F32, name="acc0")
+        LAST = len(RUNS) + 1
+        low_end = run_of(LOW_BLOCKS - 1) + 2
+        node_end = run_of(NODE_BLOCKS - 1) + 2
+        high_end = run_of(HIGH_BLOCKS - 1) + 2
+        waiting = []
+        ordered_of = {}
 
-        for h in range(2):
-            reorder(order[0], h)
-            reorder(order[1], h)
-        refill()
-        refill()
+        def reorder_block(b):
+            key, j, place = blocks[b]
+            reorder(key, j)
+            ordered_of[b] = reordered[-1]
+            if j == 1:
+                refill(1)
 
-        LOW = PASSES
-        NODE_END = LOW + 3 * (PASSES // 4) + 1
-        TOTAL = len(runs)
-        pending = []
-        fwd_step = {}
-        for a in range(TYPES):
-            fwd_step[NODE_END - 3 + a] = a
+        def reorder_run(n):
+            return list(range(starts[n], starts[n + 1])) if n < len(RUNS) else []
 
-        for n in range(TOTAL + 2):
-            if n - 1 in fwd_step:
-                quantise_fwd(fwd_step[n - 1])
-            for grouped, codes, scales in pending:
-                quantise(grouped[:], codes, scales)
-            pending = []
-            if n < TOTAL:
-                for pairs, w_pass, place in runs[n][0]:
-                    grouped = transpose_block(pairs)
-                    if place is None:
-                        codes, scales = columns(w_edge, w_pass * HIDDEN, HIDDEN)
-                    else:
-                        codes, scales = place["codes"] = new_codes()
-                    pending.append((grouped, codes, scales))
-            e = n - NODE_END
+        def transpose_run(n):
+            for b in range(starts[n], starts[n + 1]):
+                place = blocks[b][2]
+                grouped = transpose_block(ordered_of[b][:].bitcast(F32))
+                if "codes" not in place:
+                    place["codes"] = new_codes()
+                waiting.append((grouped, place["codes"]))
+
+        for b in reorder_run(0):
+            reorder_block(b)
+        for n in range(LAST + 1):
+            quantises = list(waiting)
+            waiting.clear()
+            reorders = reorder_run(n + 1)
+            if n < len(RUNS):
+                transpose_run(n)
+            for i in range(max(len(quantises), len(reorders))):
+                if i < len(quantises):
+                    grouped, codes = quantises[i]
+                    quantise(grouped[:], codes[0], codes[1])
+                if i < len(reorders):
+                    reorder_block(reorders[i])
+            e = n - node_end
             if e == 1:
-                add_agg(0)
-                add_agg(1)
-            if e == 2:
-                add_agg(2)
-                add_agg(3)
-            if e == 3:
-                add_agg(4)
-            if e == 5:
-                add_agg(5)
-                add_agg(6)
-            reorder_next()
-            if n in fwd_step:
-                interleave_fwd(fwd_step[n])
+                for a in range(4):
+                    add_agg(a)
+            for a in FWD_QUANTISE.get(e, ()):
+                quantise_fwd(a)
+            for a in FWD_INTERLEAVE.get(e, ()):
+                interleave_fwd(a)
             if e == 2:
                 quantise_agg((0, 1))
-            if e == 3:
                 quantise_agg((2, 3))
-            if e == 4:
+                add_agg(4)
+            if e == 3:
                 quantise_agg((4,))
             if n >= 2:
-                runs[n - 2][1]()
-            if n == LOW:
+                for b in range(starts[n - 2], starts[n - 1]):
+                    if b in units:
+                        units[b]()
+            if n == low_end - 1:
                 bank = bank_pool.tile([P, BANK], F32, name="bank")
                 nc.tensor.matmul(bank[:], lhsT=ones[:], rhs=bias_rows[:], start=True, stop=True)
                 nc.scalar.copy(out=bias[:], in_=bank[:])
-            if n == LOW + 1:
+            if n == low_end:
                 park()
-            if e == 0:
+            if n == node_end:
                 add_node()
-            if e == 1:
-                transpose_agg((0, 1), agg_bank())
-            if e == 2:
-                transpose_agg((2, 3), agg_bank())
-            if e == 3:
+            if n == node_end + 1:
+                transpose_agg((0, 1))
+                transpose_agg((2, 3))
+            if n == node_end + 2:
                 second_product((0, 1))
-                transpose_agg((4,), agg_bank())
-            if e == 4:
+                transpose_agg((4,))
+            if n == high_end:
                 second_product((2, 3))
-            if e == 5:
                 second_product((4,))
-                transpose_agg((5, 6), agg_bank())
-                quantise_agg((5, 6))
-            if e == 6:
+                add_agg(5)
+                add_agg(6)
+            if n == LAST:
                 add_agg(7)
+                transpose_agg((5, 6))
+                quantise_agg((5, 6))
+                transpose_agg((7,))
                 second_product((5, 6))
-                transpose_agg((7,), agg_bank())
                 quantise_agg((7,))
                 second_product((7,))

@@ -230,7 +230,7 @@ def tile_attributegnn_pa_k_kernel(
                 edges = {}
                 block(("last", c), h, edges, type_passes, 7, 1, edges, 8 * c + 4 * h)
 
-        RUNS = [1, 1, 2, 2, 2] + [3] * 8 + [3] * 8 + [3] * 4
+        RUNS = [2] * 34
         FWD_VECTOR = (1, 3)
         FWD_INTERLEAVE = {1: (0, 1), 2: (2, 3, 4), 3: (5, 6, 7)}
         FWD_QUANTISE = {2: (0, 1), 3: (2, 3, 4), 4: (5, 6, 7)}

@@ -25,7 +25,7 @@ SHARE = 32
 HALF_SHARE = SHARE // 2
 BLOCK = 4 * K_PASS
 PIECE = 2 * BLOCK
-RAW_BUFS = 9
+RAW_BUFS = 8
 
 FLOPS = 2 * FEATURES * HIDDEN * (NODES + NODES * TYPES) + 2 * TYPES * NODES * HIDDEN * REP
 
@@ -37,10 +37,11 @@ def tile_attributegnn_pa_k_kernel(
     with ExitStack() as ctx:
         keep = ctx.enter_context(tc.tile_pool(name="keep", bufs=1))
         raw_pool = ctx.enter_context(tc.tile_pool(name="raw", bufs=RAW_BUFS))
-        ordered_pool = ctx.enter_context(tc.tile_pool(name="ordered", bufs=7))
-        grouped_pool = ctx.enter_context(tc.tile_pool(name="grouped", bufs=6))
-        codes_pool = ctx.enter_context(tc.tile_pool(name="codes", bufs=12))
+        ordered_pool = ctx.enter_context(tc.tile_pool(name="ordered", bufs=5))
+        grouped_pool = ctx.enter_context(tc.tile_pool(name="grouped", bufs=4))
+        codes_pool = ctx.enter_context(tc.tile_pool(name="codes", bufs=14))
         small_pool = ctx.enter_context(tc.tile_pool(name="small", bufs=2))
+        fwd_raw_pool = ctx.enter_context(tc.tile_pool(name="fwd_raw", bufs=2))
         fwd_pool = ctx.enter_context(tc.tile_pool(name="fwd", bufs=3))
         acc_pool = ctx.enter_context(tc.psum_pool(name="acc", bufs=1))
         bank_pool = ctx.enter_context(tc.psum_pool(name="bank", bufs=4))
@@ -75,19 +76,23 @@ def tile_attributegnn_pa_k_kernel(
             cols = slice(c * 4 * K_PASS, (c + 1) * 4 * K_PASS)
             image = image_features[:, cols].rearrange("b (o k) -> b o k", o=1)
             piece(("node", c), image, edge_attributes[:, 4:5, cols])
-            for m in (2 * c, 2 * c + 1):
-                piece(("w_src", m), w_rows[:, :, m * 2 * K_PASS : (m + 1) * 2 * K_PASS])
-        for c in range(PASSES // 4):
-            piece(("high", c), edge_attributes[:, 5:7, c * 4 * K_PASS : (c + 1) * 4 * K_PASS])
-        for c in range(PASSES // 8):
-            piece(("last", c), edge_attributes[:, 7:8, c * 8 * K_PASS : (c + 1) * 8 * K_PASS])
-        for h in range(2):
-            piece(("fwd", h), fwd_rows[:, h * TYPES // 2 : (h + 1) * TYPES // 2])
+            piece(("w_src", 2 * c), w_rows[:, :, (4 * c) * K_PASS : (4 * c + 2) * K_PASS])
+            if c % 2 == 0:
+                piece(("five", c // 2), edge_attributes[:, 5:6, c * 4 * K_PASS : (c + 2) * 4 * K_PASS])
+            piece(("w_src", 2 * c + 1), w_rows[:, :, (4 * c + 2) * K_PASS : (4 * c + 4) * K_PASS])
+            if c in (1, 2):
+                piece(("fwd", c - 1), fwd_rows[:, (c - 1) * TYPES // 2 : c * TYPES // 2])
+        for a in (6, 7):
+            for c in range(PASSES // 8):
+                piece((a, c), edge_attributes[:, a : a + 1, c * 8 * K_PASS : (c + 1) * 8 * K_PASS])
 
         raws = {}
 
         def load_piece(key):
-            raw = raw_pool.tile([P, PIECE], BF16, name="raw")
+            if key[0] == "fwd":
+                raw = fwd_raw_pool.tile([P, PIECE], BF16, name="fwd_raw")
+            else:
+                raw = raw_pool.tile([P, PIECE], BF16, name="raw")
             raws[key] = raw
             parts = 2 if halved[key] else 1
             tiles = sum(view.shape[1] for view in sources[key])
@@ -107,6 +112,8 @@ def tile_attributegnn_pa_k_kernel(
             for together in zip(*dmas):
                 for target, source in together:
                     nc.sync.dma_start(out=target, in_=source)
+            if len(raws) < len(order) and order[len(raws)][0] == "fwd":
+                refill(1)
 
         refill(2)
         refill(2)
@@ -188,22 +195,20 @@ def tile_attributegnn_pa_k_kernel(
             accumulate(a, slot, edge, columns(w_edge, g * HIDDEN, HIDDEN), g)
 
         blocks = []
-        units = {}
+        units = []
 
         def low_pass(g, edges):
-            for a in range(4):
-                edge_pass(a, a, columns(edges["codes"], a * P, P), g)
+            return [lambda a=a: edge_pass(a, a, columns(edges["codes"], a * P, P), g) for a in range(4)]
 
         def type_passes(a, slot, codes, first):
-            for j in range(PACK):
-                edge_pass(a, slot, columns(codes["codes"], j * P, P), first + j)
+            return [lambda j=j: edge_pass(a, slot, columns(codes["codes"], j * P, P), first + j) for j in range(PACK)]
 
         def node_pass(g, images, ws):
-            accumulate("node", 0, columns(images["codes"], g % 4 * P, P), ws["codes"], g)
+            return [lambda: accumulate("node", 0, columns(images["codes"], g % 4 * P, P), ws["codes"], g)]
 
         def block(key, j, place, unit, *args):
             if unit is not None:
-                units[len(blocks)] = lambda: unit(*args)
+                units.extend((len(blocks), f) for f in unit(*args))
             blocks.append((key, j, place))
 
         for g in range(PASSES):
@@ -214,30 +219,29 @@ def tile_attributegnn_pa_k_kernel(
         for c in range(PASSES // 4):
             images = {}
             fours = {}
+            fives = {}
+            ws = [{}, {}, {}, {}]
             block(("node", c), 0, images, None)
             block(("node", c), 1, fours, type_passes, 4, 1, fours, 4 * c)
-            for g in range(4 * c, 4 * c + 4):
-                ws = {}
-                block(("w_src", g // 2), g % 2, ws, node_pass, g, images, ws)
+            block(("w_src", 2 * c), 0, ws[0], node_pass, 4 * c, images, ws[0])
+            block(("five", c // 2), c % 2, fives, type_passes, 5, 2, fives, 4 * c)
+            block(("w_src", 2 * c), 1, ws[1], node_pass, 4 * c + 1, images, ws[1])
+            block(("w_src", 2 * c + 1), 0, ws[2], node_pass, 4 * c + 2, images, ws[2])
+            block(("w_src", 2 * c + 1), 1, ws[3], node_pass, 4 * c + 3, images, ws[3])
         NODE_BLOCKS = len(blocks)
-        for c in range(PASSES // 4):
-            for s in range(2):
+        for a in (6, 7):
+            for c in range(PASSES // 4):
                 edges = {}
-                block(("high", c), s, edges, type_passes, 5 + s, 2 + s, edges, 4 * c)
-        HIGH_BLOCKS = len(blocks)
-        for c in range(PASSES // 8):
-            for h in range(2):
-                edges = {}
-                block(("last", c), h, edges, type_passes, 7, 1, edges, 8 * c + 4 * h)
+                block((a, c // 2), c % 2, edges, type_passes, a, 3 if a == 6 else 1, edges, 4 * c)
 
-        RUNS = [2] * 34
-        FWD_VECTOR = (1, 3)
-        FWD_INTERLEAVE = {1: (0, 1), 2: (2, 3, 4), 3: (5, 6, 7)}
-        FWD_QUANTISE = {2: (0, 1), 3: (2, 3, 4), 4: (5, 6, 7)}
-        starts = [sum(RUNS[:n]) for n in range(len(RUNS) + 1)]
+        RUN = 2
+        FWD_VECTOR = (1, 3, 5)
+        FWD_STEPS = (20, 21, 22, 23, 25, 26, 28, 30)
+        starts = list(range(0, len(blocks) + 1, RUN))
+        RUNS = len(blocks) // RUN
 
         def run_of(b):
-            return max(n for n in range(len(RUNS)) if starts[n] <= b)
+            return b // RUN
 
         parked = [keep.tile([P, HIDDEN], F32, name="park%d" % a) for a in range(4)]
         bias = keep.tile([P, HIDDEN], F32, name="bias")
@@ -320,22 +324,22 @@ def tile_attributegnn_pa_k_kernel(
             fwd_cols = columns(fwd, a * REP, REP)
             quantise(fwd_grouped[a][:], fwd_cols[0], fwd_cols[1])
 
-        LAST = len(RUNS) + 1
+        LAST = RUNS + 1
         low_end = run_of(LOW_BLOCKS - 1) + 2
         node_end = run_of(NODE_BLOCKS - 1) + 2
-        high_end = run_of(HIGH_BLOCKS - 1) + 2
         waiting = []
         ordered_of = {}
+        issued = []
 
         def reorder_block(b):
             key, j, place = blocks[b]
             reorder(key, j)
             ordered_of[b] = reordered[-1]
-            if j == 1:
+            if all(ordered_of.get(i) is not None for i in range(len(blocks)) if blocks[i][0] == key):
                 refill(1)
 
         def reorder_run(n):
-            return list(range(starts[n], starts[n + 1])) if n < len(RUNS) else []
+            return list(range(starts[n], starts[n + 1])) if n < RUNS else []
 
         def transpose_run(n):
             for b in range(starts[n], starts[n + 1]):
@@ -345,13 +349,21 @@ def tile_attributegnn_pa_k_kernel(
                     place["codes"] = new_codes()
                 waiting.append((grouped, place["codes"]))
 
+        def multiply(n):
+            k = n - low_end - 1
+            most = (3 if k % 7 < 4 else 4) if low_end < n < node_end else len(units)
+            for i in range(most):
+                if len(issued) < len(units) and units[len(issued)][0] < starts[n - 1]:
+                    units[len(issued)][1]()
+                    issued.append(n)
+
         for b in reorder_run(0):
             reorder_block(b)
         for n in range(LAST + 1):
             quantises = list(waiting)
             waiting.clear()
             reorders = reorder_run(n + 1)
-            if n < len(RUNS):
+            if n < RUNS:
                 transpose_run(n)
             for i in range(max(len(quantises), len(reorders))):
                 if i < len(quantises):
@@ -360,47 +372,46 @@ def tile_attributegnn_pa_k_kernel(
                 if i < len(reorders):
                     reorder_block(reorders[i])
             e = n - node_end
+            for a in range(TYPES):
+                if n == FWD_STEPS[a] + 1:
+                    quantise_fwd(a)
+                if n == FWD_STEPS[a]:
+                    interleave_fwd(a)
             if e == 1:
-                for a in range(4):
+                for a in (0, 1, 2):
                     add_agg(a)
-            for a in FWD_QUANTISE.get(e, ()):
-                quantise_fwd(a)
-            for a in FWD_INTERLEAVE.get(e, ()):
-                interleave_fwd(a)
             if e == 2:
                 quantise_agg((0, 1))
-                quantise_agg((2, 3))
-                add_agg(4)
+                for a in (3, 4, 5):
+                    add_agg(a)
             if e == 3:
-                quantise_agg((4,))
+                quantise_agg((2, 3))
+                quantise_agg((4, 5))
+                add_agg(6)
             if n >= 2:
-                for b in range(starts[n - 2], starts[n - 1]):
-                    if b in units:
-                        units[b]()
+                multiply(n)
             if n == low_end - 1:
                 bank = bank_pool.tile([P, BANK], F32, name="bank")
                 nc.tensor.matmul(bank[:], lhsT=ones[:], rhs=bias_rows[:], start=True, stop=True)
                 nc.scalar.copy(out=bias[:], in_=bank[:])
             if n == low_end:
                 park()
-            if n == node_end:
+            if e == 0:
                 add_node()
-            if n == node_end + 1:
+            if e == 1:
                 transpose_agg((0, 1))
-                transpose_agg((2, 3))
-            if n == node_end + 2:
+            if e == 2:
                 second_product((0, 1))
-                transpose_agg((4,))
-            if n == high_end:
+                transpose_agg((2, 3))
+                transpose_agg((4, 5))
+            if e == 3:
                 second_product((2, 3))
-                second_product((4,))
-                add_agg(5)
-                add_agg(6)
-            if n == LAST:
+                second_product((4, 5))
+            if e == 4:
                 add_agg(7)
-                transpose_agg((5, 6))
-                quantise_agg((5, 6))
+                transpose_agg((6,))
+                quantise_agg((6,))
                 transpose_agg((7,))
-                second_product((5, 6))
+                second_product((6,))
                 quantise_agg((7,))
                 second_product((7,))

@@ -37,20 +37,23 @@ def tile_attributegnn_pa_k_kernel(
     with ExitStack() as ctx:
         keep = ctx.enter_context(tc.tile_pool(name="keep", bufs=1))
         raw_pool = ctx.enter_context(tc.tile_pool(name="raw", bufs=RAW_BUFS))
-        ordered_pool = ctx.enter_context(tc.tile_pool(name="ordered", bufs=5))
+        ordered_pool = ctx.enter_context(tc.tile_pool(name="ordered", bufs=4))
         grouped_pool = ctx.enter_context(tc.tile_pool(name="grouped", bufs=4))
-        codes_pool = ctx.enter_context(tc.tile_pool(name="codes", bufs=14))
-        small_pool = ctx.enter_context(tc.tile_pool(name="small", bufs=2))
+        codes_pool = ctx.enter_context(tc.tile_pool(name="codes", bufs=12))
+        small_pool = ctx.enter_context(tc.tile_pool(name="small", bufs=3))
         fwd_raw_pool = ctx.enter_context(tc.tile_pool(name="fwd_raw", bufs=2))
+        result_pool = ctx.enter_context(tc.tile_pool(name="result", bufs=4))
         fwd_pool = ctx.enter_context(tc.tile_pool(name="fwd", bufs=3))
         acc_pool = ctx.enter_context(tc.psum_pool(name="acc", bufs=1))
         bank_pool = ctx.enter_context(tc.psum_pool(name="bank", bufs=4))
         ctx.enter_context(tc.manual_schedule())
 
         bias_rows = keep.tile([P, HIDDEN], BF16, name="bias_rows")
-        nc.gpsimd.memset(bias_rows[:], 0.0)
         ones = keep.tile([P, P], BF16, name="ones")
         nc.gpsimd.memset(ones[:], 1.0)
+        idle_rows = keep.tile([P, HIDDEN], BF16, name="idle_rows")
+        nc.gpsimd.memset(idle_rows[:], 1.0)
+        nc.gpsimd.memset(bias_rows[:], 0.0)
         nc.scalar.dma_start(out=bias_rows[0:1, :], in_=linear_b.rearrange("(o k) -> o k", o=1))
         identity = keep.tile([P, P], F32, name="identity")
         make_identity(nc, identity[:])
@@ -72,16 +75,18 @@ def tile_attributegnn_pa_k_kernel(
             piece(("w_edge", m), w_rows[:, :, FEATURES + m * 2 * K_PASS : FEATURES + (m + 1) * 2 * K_PASS])
             piece(("low", m), edge_attributes[:, 0:4, cols])
             halved["w_edge", m] = halved["low", m] = m < 2
+            if m == 4:
+                piece(("fwd", 0), fwd_rows[:, 0 : TYPES // 2])
         for c in range(PASSES // 4):
             cols = slice(c * 4 * K_PASS, (c + 1) * 4 * K_PASS)
             image = image_features[:, cols].rearrange("b (o k) -> b o k", o=1)
             piece(("node", c), image, edge_attributes[:, 4:5, cols])
             piece(("w_src", 2 * c), w_rows[:, :, (4 * c) * K_PASS : (4 * c + 2) * K_PASS])
+            piece(("w_src", 2 * c + 1), w_rows[:, :, (4 * c + 2) * K_PASS : (4 * c + 4) * K_PASS])
             if c % 2 == 0:
                 piece(("five", c // 2), edge_attributes[:, 5:6, c * 4 * K_PASS : (c + 2) * 4 * K_PASS])
-            piece(("w_src", 2 * c + 1), w_rows[:, :, (4 * c + 2) * K_PASS : (4 * c + 4) * K_PASS])
-            if c in (1, 2):
-                piece(("fwd", c - 1), fwd_rows[:, (c - 1) * TYPES // 2 : c * TYPES // 2])
+            if c == 0:
+                piece(("fwd", 1), fwd_rows[:, TYPES // 2 : TYPES])
         for a in (6, 7):
             for c in range(PASSES // 8):
                 piece((a, c), edge_attributes[:, a : a + 1, c * 8 * K_PASS : (c + 1) * 8 * K_PASS])
@@ -193,6 +198,8 @@ def tile_attributegnn_pa_k_kernel(
 
         def edge_pass(a, slot, edge, g):
             accumulate(a, slot, edge, columns(w_edge, g * HIDDEN, HIDDEN), g)
+            if a < 4 and g == PASSES - 1:
+                park(a)
 
         blocks = []
         units = []
@@ -222,21 +229,21 @@ def tile_attributegnn_pa_k_kernel(
             fives = {}
             ws = [{}, {}, {}, {}]
             block(("node", c), 0, images, None)
-            block(("node", c), 1, fours, type_passes, 4, 1, fours, 4 * c)
             block(("w_src", 2 * c), 0, ws[0], node_pass, 4 * c, images, ws[0])
-            block(("five", c // 2), c % 2, fives, type_passes, 5, 2, fives, 4 * c)
+            block(("node", c), 1, fours, type_passes, 4, 1, fours, 4 * c)
             block(("w_src", 2 * c), 1, ws[1], node_pass, 4 * c + 1, images, ws[1])
             block(("w_src", 2 * c + 1), 0, ws[2], node_pass, 4 * c + 2, images, ws[2])
+            block(("five", c // 2), c % 2, fives, type_passes, 5, 2, fives, 4 * c)
             block(("w_src", 2 * c + 1), 1, ws[3], node_pass, 4 * c + 3, images, ws[3])
         NODE_BLOCKS = len(blocks)
         for a in (6, 7):
             for c in range(PASSES // 4):
                 edges = {}
-                block((a, c // 2), c % 2, edges, type_passes, a, 3 if a == 6 else 1, edges, 4 * c)
+                block((a, c // 2), c % 2, edges, type_passes, a, 3 if a == 6 else 0, edges, 4 * c)
 
         RUN = 2
-        FWD_VECTOR = (1, 3, 5)
-        FWD_STEPS = (20, 21, 22, 23, 25, 26, 28, 30)
+        FWD_VECTOR = {3: 12, 7: 24}
+        FWD_FIRST = 9
         starts = list(range(0, len(blocks) + 1, RUN))
         RUNS = len(blocks) // RUN
 
@@ -247,12 +254,11 @@ def tile_attributegnn_pa_k_kernel(
         bias = keep.tile([P, HIDDEN], F32, name="bias")
         node_bias = keep.tile([P, HIDDEN], F32, name="node_bias")
 
-        def park():
-            for a in range(4):
-                if a % 2 == 0:
-                    nc.scalar.copy(out=parked[a][:], in_=acc[a][:])
-                else:
-                    nc.vector.tensor_copy(out=parked[a][:], in_=acc[a][:])
+        def park(a):
+            if a % 2 == 0:
+                nc.scalar.copy(out=parked[a][:], in_=acc[a][:])
+            else:
+                nc.vector.tensor_copy(out=parked[a][:], in_=acc[a][:])
 
         def add_node():
             nc.vector.tensor_tensor(out=node_bias[:], in0=acc["node"][:], in1=bias[:], op=mybir.AluOpType.add)
@@ -264,7 +270,12 @@ def tile_attributegnn_pa_k_kernel(
         def add_agg(a):
             agg[a] = small_pool.tile([P, HIDDEN], BF16, name="agg%d" % (a % 2))
             source = parked[a] if a < 4 else acc[a]
-            nc.vector.tensor_tensor(out=agg[a][:], in0=source[:], in1=node_bias[:], op=mybir.AluOpType.add)
+            nc.vector.tensor_tensor(
+                out=agg[a][:].rearrange("p (c m e) -> p c m e", c=2, e=2),
+                in0=source[:].rearrange("p (m c e) -> p c m e", c=2, e=2),
+                in1=node_bias[:].rearrange("p (m c e) -> p c m e", c=2, e=2),
+                op=mybir.AluOpType.add,
+            )
 
         def transpose_agg(types):
             n = len(types)
@@ -274,7 +285,7 @@ def tile_attributegnn_pa_k_kernel(
                 for u in range(2):
                     quarter = 2 * s + u
                     nc.tensor.transpose(
-                        bank[:, quarter * P : (quarter + 1) * P], words[:, u : HIDDEN // 2 : 2], identity[:]
+                        bank[:, quarter * P : (quarter + 1) * P], words[:, u * P : (u + 1) * P], identity[:]
                     )
             grouped = small_pool.tile([P, 2 * PACK * P], BF16, name="agg_grouped", align_bytes=64)
             agg_grouped[types] = grouped
@@ -290,7 +301,7 @@ def tile_attributegnn_pa_k_kernel(
             agg_codes[types] = (codes, scales)
             quantise(agg_grouped[types][:, 0 : n * PACK * P], codes[:, 0 : n * P], scales[:, 0 : n * P])
 
-        def second_product(types):
+        def second_product(types, copy=nc.scalar.copy):
             n = len(types)
             bank = bank_pool.tile([P, BANK], F32, name="bank")
             for s in range(n):
@@ -301,8 +312,8 @@ def tile_attributegnn_pa_k_kernel(
                     True,
                     True,
                 )
-            result = small_pool.tile([P, BANK], F32, name="result")
-            nc.scalar.copy(out=result[:, 0 : n * REP], in_=bank[:, 0 : n * REP])
+            result = result_pool.tile([P, BANK], F32, name="result")
+            copy(out=result[:, 0 : n * REP], in_=bank[:, 0 : n * REP])
             nc.sync.dma_start(
                 out=out[:, types[0] : types[0] + n, :],
                 in_=result[:, 0 : n * REP].rearrange("b (a r) -> b a r", a=n),
@@ -310,15 +321,17 @@ def tile_attributegnn_pa_k_kernel(
 
         fwd_grouped = {}
 
-        def interleave_fwd(a):
-            fwd_grouped[a] = fwd_pool.tile([P, PACK * REP], BF16, name="fwd_grouped", align_bytes=64)
-            target = fwd_grouped[a][:].rearrange("p (r t) -> p r t", t=PACK)
+        def interleave_fwd(a, quarter):
+            if quarter == 0:
+                fwd_grouped[a] = fwd_pool.tile([P, PACK * REP], BF16, name="fwd_grouped", align_bytes=64)
             h, i = divmod(a, TYPES // 2)
-            source = raws["fwd", h][:, i * PACK * REP : (i + 1) * PACK * REP].rearrange("p (t r) -> p r t", t=PACK)
-            if a not in FWD_VECTOR:
-                nc.scalar.copy(out=target, in_=source)
-            else:
+            reps = slice(quarter * REP // 4, (quarter + 1) * REP // 4)
+            target = fwd_grouped[a][:].rearrange("p (r t) -> p r t", t=PACK)[:, reps]
+            source = raws["fwd", h][:, i * PACK * REP : (i + 1) * PACK * REP].rearrange("p (t r) -> p r t", t=PACK)[:, reps]
+            if a in FWD_VECTOR:
                 nc.vector.tensor_copy(out=target, in_=source)
+            else:
+                nc.scalar.copy(out=target, in_=source)
 
         def quantise_fwd(a):
             fwd_cols = columns(fwd, a * REP, REP)
@@ -330,6 +343,7 @@ def tile_attributegnn_pa_k_kernel(
         waiting = []
         ordered_of = {}
         issued = []
+        fwd_scalar = [a for a in range(TYPES) if a not in FWD_VECTOR]
 
         def reorder_block(b):
             key, j, place = blocks[b]
@@ -348,18 +362,27 @@ def tile_attributegnn_pa_k_kernel(
                 if "codes" not in place:
                     place["codes"] = new_codes()
                 waiting.append((grouped, place["codes"]))
+                if b < 4:
+                    keep_clock(2)
+
+        paced = max(i for i in range(len(units)) if units[i][0] < NODE_BLOCKS) + 1
 
         def multiply(n):
-            k = n - low_end - 1
-            most = (3 if k % 7 < 4 else 4) if low_end < n < node_end else len(units)
-            for i in range(most):
-                if len(issued) < len(units) and units[len(issued)][0] < starts[n - 1]:
-                    units[len(issued)][1]()
-                    issued.append(n)
+            most = paced * n // node_end if n < node_end else len(units)
+            while len(issued) < most and units[len(issued)][0] < starts[min(n, RUNS)]:
+                units[len(issued)][1]()
+                issued.append(n)
 
+        warm_bank = acc_pool.tile([P, BANK], F32, name="acc3")
+
+        def keep_clock(count):
+            for i in range(count):
+                nc.tensor.matmul(warm_bank[:], lhsT=ones[:], rhs=idle_rows[:], start=True, stop=True)
+
+        keep_clock(8)
         for b in reorder_run(0):
             reorder_block(b)
-        for n in range(LAST + 1):
+        for n in range(LAST):
             quantises = list(waiting)
             waiting.clear()
             reorders = reorder_run(n + 1)
@@ -372,30 +395,32 @@ def tile_attributegnn_pa_k_kernel(
                 if i < len(reorders):
                     reorder_block(reorders[i])
             e = n - node_end
-            for a in range(TYPES):
-                if n == FWD_STEPS[a] + 1:
+            if FWD_FIRST <= n < FWD_FIRST + 4 * len(fwd_scalar):
+                i, quarter = divmod(n - FWD_FIRST, 4)
+                interleave_fwd(fwd_scalar[i], quarter)
+            for a in FWD_VECTOR:
+                if 0 <= n - FWD_VECTOR[a] < 4:
+                    interleave_fwd(a, n - FWD_VECTOR[a])
+                if n - FWD_VECTOR[a] == 5:
                     quantise_fwd(a)
-                if n == FWD_STEPS[a]:
-                    interleave_fwd(a)
+            if n > FWD_FIRST and (n - FWD_FIRST) % 4 == 0 and (n - FWD_FIRST) // 4 <= len(fwd_scalar):
+                quantise_fwd(fwd_scalar[(n - FWD_FIRST) // 4 - 1])
             if e == 1:
                 for a in (0, 1, 2):
                     add_agg(a)
             if e == 2:
                 quantise_agg((0, 1))
-                for a in (3, 4, 5):
+                for a in (3, 4, 5, 6):
                     add_agg(a)
             if e == 3:
                 quantise_agg((2, 3))
                 quantise_agg((4, 5))
-                add_agg(6)
-            if n >= 2:
-                multiply(n)
+                quantise_agg((6,))
+            multiply(n)
             if n == low_end - 1:
                 bank = bank_pool.tile([P, BANK], F32, name="bank")
                 nc.tensor.matmul(bank[:], lhsT=ones[:], rhs=bias_rows[:], start=True, stop=True)
                 nc.scalar.copy(out=bias[:], in_=bank[:])
-            if n == low_end:
-                park()
             if e == 0:
                 add_node()
             if e == 1:
@@ -404,14 +429,12 @@ def tile_attributegnn_pa_k_kernel(
                 second_product((0, 1))
                 transpose_agg((2, 3))
                 transpose_agg((4, 5))
-            if e == 3:
-                second_product((2, 3))
-                second_product((4, 5))
-            if e == 4:
-                add_agg(7)
                 transpose_agg((6,))
-                quantise_agg((6,))
+            if e == 3:
+                add_agg(7)
+                second_product((2, 3))
+                second_product((4, 5), nc.vector.tensor_copy)
                 transpose_agg((7,))
-                second_product((6,))
                 quantise_agg((7,))
+                second_product((6,))
                 second_product((7,))

@@ -51,8 +51,6 @@ def tile_attributegnn_pa_k_kernel(
         bias_rows = keep.tile([P, HIDDEN], BF16, name="bias_rows")
         ones = keep.tile([P, P], BF16, name="ones")
         nc.gpsimd.memset(ones[:], 1.0)
-        idle_rows = keep.tile([P, HIDDEN], BF16, name="idle_rows")
-        nc.gpsimd.memset(idle_rows[:], 1.0)
         nc.gpsimd.memset(bias_rows[:], 0.0)
         nc.scalar.dma_start(out=bias_rows[0:1, :], in_=linear_b.rearrange("(o k) -> o k", o=1))
         identity = keep.tile([P, P], F32, name="identity")
@@ -74,7 +72,7 @@ def tile_attributegnn_pa_k_kernel(
             cols = slice(m * 2 * K_PASS, (m + 1) * 2 * K_PASS)
             piece(("w_edge", m), w_rows[:, :, FEATURES + m * 2 * K_PASS : FEATURES + (m + 1) * 2 * K_PASS])
             piece(("low", m), edge_attributes[:, 0:4, cols])
-            halved["w_edge", m] = halved["low", m] = m < 2
+            halved["w_edge", m] = halved["low", m] = m < 1
             if m == 4:
                 piece(("fwd", 0), fwd_rows[:, 0 : TYPES // 2])
         for c in range(PASSES // 4):
@@ -121,8 +119,7 @@ def tile_attributegnn_pa_k_kernel(
                 refill(1)
 
         refill(2)
-        refill(2)
-        for i in range(RAW_BUFS - 4):
+        for i in range(RAW_BUFS - 2):
             refill(1)
 
         def raw_block(key, j):
@@ -362,8 +359,6 @@ def tile_attributegnn_pa_k_kernel(
                 if "codes" not in place:
                     place["codes"] = new_codes()
                 waiting.append((grouped, place["codes"]))
-                if b < 4:
-                    keep_clock(2)
 
         paced = max(i for i in range(len(units)) if units[i][0] < NODE_BLOCKS) + 1
 
@@ -373,13 +368,6 @@ def tile_attributegnn_pa_k_kernel(
                 units[len(issued)][1]()
                 issued.append(n)
 
-        warm_bank = acc_pool.tile([P, BANK], F32, name="acc3")
-
-        def keep_clock(count):
-            for i in range(count):
-                nc.tensor.matmul(warm_bank[:], lhsT=ones[:], rhs=idle_rows[:], start=True, stop=True)
-
-        keep_clock(8)
         for b in reorder_run(0):
             reorder_block(b)
         for n in range(LAST):
@@ -417,7 +405,7 @@ def tile_attributegnn_pa_k_kernel(
                 quantise_agg((4, 5))
                 quantise_agg((6,))
             multiply(n)
-            if n == low_end - 1:
+            if n == 4:
                 bank = bank_pool.tile([P, BANK], F32, name="bank")
                 nc.tensor.matmul(bank[:], lhsT=ones[:], rhs=bias_rows[:], start=True, stop=True)
                 nc.scalar.copy(out=bias[:], in_=bank[:])

from contextlib import ExitStack

import concourse.mybir as mybir
from concourse.masks import make_identity

F32 = mybir.dt.float32
BF16 = mybir.dt.bfloat16
U32 = mybir.dt.uint32
U8 = mybir.dt.uint8
FP8X4 = mybir.dt.float8_e4m3fn_x4

NODES = 128
TYPES = 8
FEATURES = 8192
HIDDEN = 512
REP = 256

P = 128
PACK = 4
K_PASS = P * PACK
PASSES = FEATURES // K_PASS
BANK = 512

SHARE = 32
HALF_SHARE = SHARE // 2
BLOCK = 4 * K_PASS
PIECE = 2 * BLOCK
RAW_BUFS = 8

FLOPS = 2 * FEATURES * HIDDEN * (NODES + NODES * TYPES) + 2 * TYPES * NODES * HIDDEN * REP


def tile_attributegnn_pa_k_kernel(
    tc, image_features, edge_attributes, linear_w, linear_b, fwd_proj, out
):
    nc = tc.nc
    with ExitStack() as ctx:
        keep = ctx.enter_context(tc.tile_pool(name="keep", bufs=1))
        raw_pool = ctx.enter_context(tc.tile_pool(name="raw", bufs=RAW_BUFS))
        ordered_pool = ctx.enter_context(tc.tile_pool(name="ordered", bufs=4))
        grouped_pool = ctx.enter_context(tc.tile_pool(name="grouped", bufs=4))
        codes_pool = ctx.enter_context(tc.tile_pool(name="codes", bufs=12))
        small_pool = ctx.enter_context(tc.tile_pool(name="small", bufs=3))
        fwd_raw_pool = ctx.enter_context(tc.tile_pool(name="fwd_raw", bufs=2))
        result_pool = ctx.enter_context(tc.tile_pool(name="result", bufs=4))
        fwd_pool = ctx.enter_context(tc.tile_pool(name="fwd", bufs=3))
        acc_pool = ctx.enter_context(tc.psum_pool(name="acc", bufs=1))
        bank_pool = ctx.enter_context(tc.psum_pool(name="bank", bufs=4))
        ctx.enter_context(tc.manual_schedule())

        bias_rows = keep.tile([P, HIDDEN], BF16, name="bias_rows")
        ones = keep.tile([P, P], BF16, name="ones")
        nc.gpsimd.memset(ones[:], 1.0)
        nc.gpsimd.memset(bias_rows[:], 0.0)
        nc.scalar.dma_start(out=bias_rows[0:1, :], in_=linear_b.rearrange("(o k) -> o k", o=1))
        identity = keep.tile([P, P], F32, name="identity")
        make_identity(nc, identity[:])

        w_rows = linear_w.rearrange("(i p) k -> p i k", p=P)
        fwd_rows = fwd_proj.rearrange("a (p t) r -> p a (t r)", t=PACK)

        order = []
        sources = {}
        halved = {}

        def piece(key, *views):
            order.append(key)
            sources[key] = views
            halved[key] = False

        for m in range(PASSES // 2):
            cols = slice(m * 2 * K_PASS, (m + 1) * 2 * K_PASS)
            piece(("w_edge", m), w_rows[:, :, FEATURES + m * 2 * K_PASS : FEATURES + (m + 1) * 2 * K_PASS])
            piece(("low", m), edge_attributes[:, 0:4, cols])
            halved["w_edge", m] = halved["low", m] = m < 1
            if m == 4:
                piece(("fwd", 0), fwd_rows[:, 0 : TYPES // 2])
        for c in range(PASSES // 4):
            cols = slice(c * 4 * K_PASS, (c + 1) * 4 * K_PASS)
            image = image_features[:, cols].rearrange("b (o k) -> b o k", o=1)
            piece(("node", c), image, edge_attributes[:, 4:5, cols])
            piece(("w_src", 2 * c), w_rows[:, :, (4 * c) * K_PASS : (4 * c + 2) * K_PASS])
            piece(("w_src", 2 * c + 1), w_rows[:, :, (4 * c + 2) * K_PASS : (4 * c + 4) * K_PASS])
            if c % 2 == 0:
                piece(("five", c // 2), edge_attributes[:, 5:6, c * 4 * K_PASS : (c + 2) * 4 * K_PASS])
            if c == 0:
                piece(("fwd", 1), fwd_rows[:, TYPES // 2 : TYPES])
        for a in (6, 7):
            for c in range(PASSES // 8):
                piece((a, c), edge_attributes[:, a : a + 1, c * 8 * K_PASS : (c + 1) * 8 * K_PASS])

        raws = {}

        def load_piece(key):
            if key[0] == "fwd":
                raw = fwd_raw_pool.tile([P, PIECE], BF16, name="fwd_raw")
            else:
                raw = raw_pool.tile([P, PIECE], BF16, name="raw")
            raws[key] = raw
            parts = 2 if halved[key] else 1
            tiles = sum(view.shape[1] for view in sources[key])
            target = raw[:].rearrange("p (h i k) -> p h i k", h=parts, i=tiles)
            width = PIECE // (parts * tiles)
            dmas = []
            for h in range(parts):
                i = 0
                for view in sources[key]:
                    n = view.shape[1]
                    dmas.append((target[:, h, i : i + n], view[:, :, h * width : (h + 1) * width]))
                    i += n
            return dmas

        def refill(count):
            dmas = [load_piece(order[len(raws)]) for i in range(count) if len(raws) < len(order)]
            for together in zip(*dmas):
                for target, source in together:
                    nc.sync.dma_start(out=target, in_=source)
            if len(raws) < len(order) and order[len(raws)][0] == "fwd":
                refill(1)

        refill(2)
        for i in range(RAW_BUFS - 2):
            refill(1)

        def raw_block(key, j):
            raw = raws[key]
            if key[0] in ("w_edge", "low", "w_src"):
                pattern = "p (j s n u e) -> p j s n u e" if halved[key] else "p (s j n u e) -> p j s n u e"
                return raw[:].rearrange(pattern, j=2, s=4, u=2, e=HALF_SHARE)[:, j]
            return raw[:].rearrange("p (j s n u e) -> p j s n u e", j=2, s=4, u=2, e=HALF_SHARE)[:, j]

        reordered = []

        def reorder(key, j):
            ordered = ordered_pool.tile([P, BLOCK], BF16, name="ordered")
            nc.vector.tensor_copy(
                out=ordered[:].rearrange("p (u s n e) -> p u s n e", u=2, s=4, e=HALF_SHARE),
                in_=raw_block(key, j).rearrange("p s n u e -> p u s n e"),
            )
            reordered.append(ordered)

        def transpose_block(words):
            grouped = grouped_pool.tile([P, PACK * BANK], BF16, name="grouped", align_bytes=64)
            grouped_words = grouped[:].bitcast(F32)
            for half in range(2):
                bank = bank_pool.tile([P, BANK], F32, name="bank")
                for s in range(2):
                    for u in range(2):
                        quarter = 2 * s + u
                        first = (4 * u + 2 * half + s) * P
                        nc.tensor.transpose(
                            bank[:, quarter * P : (quarter + 1) * P], words[:, first : first + P], identity[:]
                        )
                nc.scalar.copy(
                    out=grouped_words[:, half * BANK : (half + 1) * BANK].rearrange("p (s r u) -> p s r u", s=2, u=2),
                    in_=bank[:].rearrange("p (s u r) -> p s r u", s=2, u=2),
                )
            return grouped

        def quantise(grouped, codes, scales):
            nc.vector.quantize_mx(out=codes.bitcast(FP8X4), scales=scales, in_=grouped)

        def new_codes():
            codes = codes_pool.tile([P, BANK], U32, name="codes", align_bytes=64)
            scales = codes_pool.tile([P, BANK], U8, name="scales", align_bytes=64)
            return codes[:], scales[:]

        def mx(bank, lhs, rhs, start, stop):
            nc.tensor.matmul_mx(
                out=bank,
                lhsT=lhs[0].bitcast(FP8X4),
                lhsT_scale=lhs[1],
                rhs=rhs[0].bitcast(FP8X4),
                rhs_scale=rhs[1],
                start=start,
                stop=stop,
            )

        def columns(pair, first, width):
            return pair[0][:, first : first + width], pair[1][:, first : first + width]

        w_edge_codes = keep.tile([P, PASSES * HIDDEN], U32, name="w_edge_codes", align_bytes=64)
        w_edge_scales = keep.tile([P, PASSES * HIDDEN], U8, name="w_edge_scales", align_bytes=64)
        w_edge = (w_edge_codes, w_edge_scales)
        fwd_codes = keep.tile([P, TYPES * REP], U32, name="fwd_codes", align_bytes=64)
        fwd_scales = keep.tile([P, TYPES * REP], U8, name="fwd_scales", align_bytes=64)
        fwd = (fwd_codes, fwd_scales)

        acc = {}

        def accumulate(name, slot, lhs, rhs, g):
            if g == 0:
                acc[name] = acc_pool.tile([P, BANK], F32, name="acc%d" % slot)
            mx(acc[name][:], lhs, rhs, g == 0, g == PASSES - 1)

        def edge_pass(a, slot, edge, g):
            accumulate(a, slot, edge, columns(w_edge, g * HIDDEN, HIDDEN), g)
            if a < 4 and g == PASSES - 1:
                park(a)

        blocks = []
        units = []

        def low_pass(g, edges):
            return [lambda a=a: edge_pass(a, a, columns(edges["codes"], a * P, P), g) for a in range(4)]

        def type_passes(a, slot, codes, first):
            return [lambda j=j: edge_pass(a, slot, columns(codes["codes"], j * P, P), first + j) for j in range(PACK)]

        def node_pass(g, images, ws):
            return [lambda: accumulate("node", 0, columns(images["codes"], g % 4 * P, P), ws["codes"], g)]

        def block(key, j, place, unit, *args):
            if unit is not None:
                units.extend((len(blocks), f) for f in unit(*args))
            blocks.append((key, j, place))

        for g in range(PASSES):
            edges = {}
            block(("w_edge", g // 2), g % 2, {"codes": columns(w_edge, g * HIDDEN, HIDDEN)}, None)
            block(("low", g // 2), g % 2, edges, low_pass, g, edges)
        LOW_BLOCKS = len(blocks)
        for c in range(PASSES // 4):
            images = {}
            fours = {}
            fives = {}
            ws = [{}, {}, {}, {}]
            block(("node", c), 0, images, None)
            block(("w_src", 2 * c), 0, ws[0], node_pass, 4 * c, images, ws[0])
            block(("node", c), 1, fours, type_passes, 4, 1, fours, 4 * c)
            block(("w_src", 2 * c), 1, ws[1], node_pass, 4 * c + 1, images, ws[1])
            block(("w_src", 2 * c + 1), 0, ws[2], node_pass, 4 * c + 2, images, ws[2])
            block(("five", c // 2), c % 2, fives, type_passes, 5, 2, fives, 4 * c)
            block(("w_src", 2 * c + 1), 1, ws[3], node_pass, 4 * c + 3, images, ws[3])
        NODE_BLOCKS = len(blocks)
        for a in (6, 7):
            for c in range(PASSES // 4):
                edges = {}
                block((a, c // 2), c % 2, edges, type_passes, a, 3 if a == 6 else 0, edges, 4 * c)

        RUN = 2
        FWD_VECTOR = {3: 12, 7: 24}
        FWD_FIRST = 9
        starts = list(range(0, len(blocks) + 1, RUN))
        RUNS = len(blocks) // RUN

        def run_of(b):
            return b // RUN

        parked = [keep.tile([P, HIDDEN], F32, name="park%d" % a) for a in range(4)]
        bias = keep.tile([P, HIDDEN], F32, name="bias")
        node_bias = keep.tile([P, HIDDEN], F32, name="node_bias")

        def park(a):
            if a % 2 == 0:
                nc.scalar.copy(out=parked[a][:], in_=acc[a][:])
            else:
                nc.vector.tensor_copy(out=parked[a][:], in_=acc[a][:])

        def add_node():
            nc.vector.tensor_tensor(out=node_bias[:], in0=acc["node"][:], in1=bias[:], op=mybir.AluOpType.add)

        agg = {}
        agg_grouped = {}
        agg_codes = {}

        def add_agg(a):
            agg[a] = small_pool.tile([P, HIDDEN], BF16, name="agg%d" % (a % 2))
            source = parked[a] if a < 4 else acc[a]
            nc.vector.tensor_tensor(
                out=agg[a][:].rearrange("p (c m e) -> p c m e", c=2, e=2),
                in0=source[:].rearrange("p (m c e) -> p c m e", c=2, e=2),
                in1=node_bias[:].rearrange("p (m c e) -> p c m e", c=2, e=2),
                op=mybir.AluOpType.add,
            )

        def transpose_agg(types):
            n = len(types)
            bank = bank_pool.tile([P, BANK], F32, name="bank")
            for s in range(n):
                words = agg[types[s]][:].bitcast(F32)
                for u in range(2):
                    quarter = 2 * s + u
                    nc.tensor.transpose(
                        bank[:, quarter * P : (quarter + 1) * P], words[:, u * P : (u + 1) * P], identity[:]
                    )
            grouped = small_pool.tile([P, 2 * PACK * P], BF16, name="agg_grouped", align_bytes=64)
            agg_grouped[types] = grouped
            nc.scalar.copy(
                out=grouped[:].bitcast(F32)[:, 0 : n * 2 * P].rearrange("p (s r u) -> p s r u", s=n, u=2),
                in_=bank[:, 0 : n * 2 * P].rearrange("p (s u r) -> p s r u", s=n, u=2),
            )

        def quantise_agg(types):
            n = len(types)
            codes = small_pool.tile([P, 2 * P], U32, name="agg_codes", align_bytes=64)
            scales = small_pool.tile([P, 2 * P], U8, name="agg_scales", align_bytes=64)
            agg_codes[types] = (codes, scales)
            quantise(agg_grouped[types][:, 0 : n * PACK * P], codes[:, 0 : n * P], scales[:, 0 : n * P])

        def second_product(types, copy=nc.scalar.copy):
            n = len(types)
            bank = bank_pool.tile([P, BANK], F32, name="bank")
            for s in range(n):
                mx(
                    bank[:, s * REP : (s + 1) * REP],
                    columns(agg_codes[types], s * P, P),
                    columns(fwd, types[s] * REP, REP),
                    True,
                    True,
                )
            result = result_pool.tile([P, BANK], F32, name="result")
            copy(out=result[:, 0 : n * REP], in_=bank[:, 0 : n * REP])
            nc.sync.dma_start(
                out=out[:, types[0] : types[0] + n, :],
                in_=result[:, 0 : n * REP].rearrange("b (a r) -> b a r", a=n),
            )

        fwd_grouped = {}

        def interleave_fwd(a, quarter):
            if quarter == 0:
                fwd_grouped[a] = fwd_pool.tile([P, PACK * REP], BF16, name="fwd_grouped", align_bytes=64)
            h, i = divmod(a, TYPES // 2)
            reps = slice(quarter * REP // 4, (quarter + 1) * REP // 4)
            target = fwd_grouped[a][:].rearrange("p (r t) -> p r t", t=PACK)[:, reps]
            source = raws["fwd", h][:, i * PACK * REP : (i + 1) * PACK * REP].rearrange("p (t r) -> p r t", t=PACK)[:, reps]
            if a in FWD_VECTOR:
                nc.vector.tensor_copy(out=target, in_=source)
            else:
                nc.scalar.copy(out=target, in_=source)

        def quantise_fwd(a):
            fwd_cols = columns(fwd, a * REP, REP)
            quantise(fwd_grouped[a][:], fwd_cols[0], fwd_cols[1])

        LAST = RUNS + 1
        low_end = run_of(LOW_BLOCKS - 1) + 2
        node_end = run_of(NODE_BLOCKS - 1) + 2
        waiting = []
        ordered_of = {}
        issued = []
        fwd_scalar = [a for a in range(TYPES) if a not in FWD_VECTOR]

        def reorder_block(b):
            key, j, place = blocks[b]
            reorder(key, j)
            ordered_of[b] = reordered[-1]
            if all(ordered_of.get(i) is not None for i in range(len(blocks)) if blocks[i][0] == key):
                refill(1)

        def reorder_run(n):
            return list(range(starts[n], starts[n + 1])) if n < RUNS else []

        def transpose_run(n):
            for b in range(starts[n], starts[n + 1]):
                place = blocks[b][2]
                grouped = transpose_block(ordered_of[b][:].bitcast(F32))
                if "codes" not in place:
                    place["codes"] = new_codes()
                waiting.append((grouped, place["codes"]))

        paced = max(i for i in range(len(units)) if units[i][0] < NODE_BLOCKS) + 1

        def multiply(n):
            most = paced * n // node_end if n < node_end else len(units)
            while len(issued) < most and units[len(issued)][0] < starts[min(n, RUNS)]:
                units[len(issued)][1]()
                issued.append(n)

        for b in reorder_run(0):
            reorder_block(b)
        for n in range(LAST):
            quantises = list(waiting)
            waiting.clear()
            reorders = reorder_run(n + 1)
            if n < RUNS:
                transpose_run(n)
            for i in range(max(len(quantises), len(reorders))):
                if i < len(quantises):
                    grouped, codes = quantises[i]
                    quantise(grouped[:], codes[0], codes[1])
                if i < len(reorders):
                    reorder_block(reorders[i])
            e = n - node_end
            if FWD_FIRST <= n < FWD_FIRST + 4 * len(fwd_scalar):
                i, quarter = divmod(n - FWD_FIRST, 4)
                interleave_fwd(fwd_scalar[i], quarter)
            for a in FWD_VECTOR:
                if 0 <= n - FWD_VECTOR[a] < 4:
                    interleave_fwd(a, n - FWD_VECTOR[a])
                if n - FWD_VECTOR[a] == 5:
                    quantise_fwd(a)
            if n > FWD_FIRST and (n - FWD_FIRST) % 4 == 0 and (n - FWD_FIRST) // 4 <= len(fwd_scalar):
                quantise_fwd(fwd_scalar[(n - FWD_FIRST) // 4 - 1])
            if e == 1:
                for a in (0, 1, 2):
                    add_agg(a)
            if e == 2:
                quantise_agg((0, 1))
                for a in (3, 4, 5, 6):
                    add_agg(a)
            if e == 3:
                quantise_agg((2, 3))
                quantise_agg((4, 5))
                quantise_agg((6,))
            multiply(n)
            if n == 4:
                bank = bank_pool.tile([P, BANK], F32, name="bank")
                nc.tensor.matmul(bank[:], lhsT=ones[:], rhs=bias_rows[:], start=True, stop=True)
                nc.scalar.copy(out=bias[:], in_=bank[:])
            if e == 0:
                add_node()
            if e == 1:
                transpose_agg((0, 1))
            if e == 2:
                second_product((0, 1))
                transpose_agg((2, 3))
                transpose_agg((4, 5))
                transpose_agg((6,))
            if e == 3:
                add_agg(7)
                second_product((2, 3))
                second_product((4, 5), nc.vector.tensor_copy)
                transpose_agg((7,))
                quantise_agg((7,))
                second_product((6,))
                second_product((7,))
